import numpy as np
import ml_dtypes


def mxq(x, axis, fmt="e4m3"):
    dtype, down = {"e4m3": (ml_dtypes.float8_e4m3fn, 7), "e5m2": (ml_dtypes.float8_e5m2, 14)}[fmt]
    v = np.moveaxis(np.asarray(x, np.float32).astype(ml_dtypes.bfloat16).astype(np.float64), axis, -1)
    blocks = v.reshape(v.shape[:-1] + (-1, 32))
    amax = np.abs(blocks).max(-1, keepdims=True)
    byte = np.maximum(np.where(amax > 0, np.frexp(amax)[1] - 1 + 127, 0) - down, 1)
    scale = np.exp2(byte - 127.0)
    codes = (blocks / scale).astype(np.float32).astype(dtype).astype(np.float64)
    return np.moveaxis((codes * scale).reshape(v.shape), -1, axis)


WIDE = False


def mx_kscale(k):
    if not WIDE:
        return np.ones(k)
    levels = np.array([10, -10, 5, -5, 0])
    a = np.random.permutation(np.resize(levels, k // 512 * 4)).reshape(k // 512, 4)
    idx = np.arange(k)
    return np.exp2(a[idx // 512, idx % 128 // 32])


BF16 = ml_dtypes.bfloat16


def bf(x):
    return np.asarray(x, np.float32).astype(BF16)


def f64(x):
    return np.asarray(x).astype(np.float64)


N, F, D1, D2, D3, D4, D5 = 2048, 64, 16, 1024, 512, 1024, 256
EDGE_PROB = 0.003
LEAKY_SLOPE = 0.01
DEG = 2.0 * EDGE_PROB * N


def sigmoid(v):
    return 1.0 / (1.0 + np.exp(-v))


def adjacency():
    u = np.random.uniform(size=(N, N))
    a = np.where(u < EDGE_PROB, 1.0, 0.0)
    return np.maximum(a, a.T)


def setup_inputs():
    s = mx_kscale(N)
    g = np.random.standard_normal((N, D4)) * 0.75
    h = np.maximum(g, LEAKY_SLOPE * g)
    return {"h4": bf(h / s[:, None]),
            "A": bf(adjacency() * s),
            "W4": bf(np.random.standard_normal((D4, D5)) * 0.8 / np.sqrt(D4 * DEG))}


def reference(h4, A, W4):
    t5 = mxq(f64(A), 1, "e4m3") @ mxq(f64(h4), 0, "e4m3")
    a5 = mxq(t5, 1, "e4m3") @ mxq(f64(W4), 0, "e4m3")
    z = sigmoid(a5)
    return t5, a5, z

@@ -1,0 +1,234 @@
+from contextlib import ExitStack
+
+import concourse.mybir as mybir
+from concourse.masks import make_identity
+
+F32 = mybir.dt.float32
+BF16 = mybir.dt.bfloat16
+U32 = mybir.dt.uint32
+U8 = mybir.dt.uint8
+FP8X4 = mybir.dt.float8_e4m3fn_x4
+
+P = 128
+PACK = 4
+K_PASS = P * PACK
+BANK = 512
+PASSES_PER_BANK = 2
+
+NODES = 2048
+FEATS = 1024
+OUTS = 256
+
+ROW_TILES = NODES // P
+NODE_PASSES = NODES // K_PASS
+FEAT_PASSES = FEATS // K_PASS
+HALVES = FEATS // BANK
+
+FLOPS = 2 * NODES * NODES * FEATS + 2 * NODES * FEATS * OUTS
+
+
+def tile_gcn_kron_pb_kernel(tc, h4, A, W4, out_0, out_1, out_2):
+    nc = tc.nc
+    with ExitStack() as ctx:
+        keep = ctx.enter_context(tc.tile_pool(name="keep", bufs=1))
+        a_in = ctx.enter_context(tc.tile_pool(name="a_in", bufs=ROW_TILES))
+        h_in = ctx.enter_context(tc.tile_pool(name="h_in", bufs=NODE_PASSES))
+        stage = ctx.enter_context(tc.tile_pool(name="stage", bufs=2))
+        ring = ctx.enter_context(tc.tile_pool(name="ring", bufs=3))
+        flip_psum = ctx.enter_context(tc.psum_pool(name="flip_psum", bufs=4))
+        t5_psum = ctx.enter_context(tc.psum_pool(name="t5_psum", bufs=3))
+        a5_psum = ctx.enter_context(tc.psum_pool(name="a5_psum", bufs=1))
+        ctx.enter_context(tc.manual_schedule())
+
+        identity = keep.tile([P, P], F32)
+        make_identity(nc, identity[:])
+
+        a_rows_of = {}
+        h_rows_of = {}
+
+        def load_a(i):
+            a_rows = a_in.tile([P, NODES], BF16)
+            nc.sync.dma_start(out=a_rows[:], in_=A[i * P : (i + 1) * P, :])
+            a_rows_of[i] = a_rows
+
+        def load_h(g):
+            h_rows = h_in.tile([P, PACK, FEATS], BF16)
+            nc.sync.dma_start(
+                out=h_rows[:].rearrange("q (u e) c -> q u e c", e=2),
+                in_=h4[g * K_PASS : (g + 1) * K_PASS, :].rearrange("(u q e) c -> q u e c", u=2, e=2),
+            )
+            h_rows_of[g] = h_rows
+
+        load_a(0)
+        for g in range(NODE_PASSES):
+            load_h(g)
+        load_a(1)
+        w_rows = keep.tile([P, FEAT_PASSES, PACK, OUTS], BF16)
+        nc.sync.dma_start(
+            out=w_rows[:].rearrange("q g (u e) n -> q (g u) e n", e=2),
+            in_=W4.rearrange("(gu q e) n -> q gu e n", q=P, e=2),
+        )
+        for i in range(2, ROW_TILES):
+            load_a(i)
+
+        h_codes = keep.tile([P, NODE_PASSES, FEATS], U32, align_bytes=64)
+        h_scales = keep.tile([P, NODE_PASSES, FEATS], U8, align_bytes=64)
+        w_codes = keep.tile([P, FEAT_PASSES, OUTS], U32, align_bytes=64)
+        w_scales = keep.tile([P, FEAT_PASSES, OUTS], U8, align_bytes=64)
+
+        def copy_part(part, out, in_):
+            if part == 0:
+                nc.vector.tensor_copy(out=out, in_=in_)
+            else:
+                nc.scalar.copy(out=out, in_=in_)
+
+        def quantise_h(g):
+            h_grouped = stage.tile([P, FEATS, PACK], BF16, align_bytes=64)
+            for half in range(HALVES):
+                cols = slice(half * BANK, (half + 1) * BANK)
+                copy_part(
+                    half,
+                    h_grouped[:, cols, :].rearrange("q (c i) t -> q c t i", i=4),
+                    h_rows_of[g][:, :, cols].rearrange("q t (c i) -> q c t i", i=4),
+                )
+            for half in range(HALVES):
+                cols = slice(half * BANK, (half + 1) * BANK)
+                nc.vector.quantize_mx(
+                    out=h_codes[:, g, cols].bitcast(FP8X4),
+                    scales=h_scales[:, g, cols],
+                    in_=h_grouped[:, cols, :].rearrange("q c t -> q (c t)"),
+                )
+
+        def quantise_w():
+            w_grouped = keep.tile([P, FEAT_PASSES, OUTS, PACK], BF16, align_bytes=64)
+            for g in range(FEAT_PASSES):
+                copy_part(g, w_grouped[:, g, :, :], w_rows[:, g, :, :].rearrange("q t n -> q n t"))
+            nc.vector.quantize_mx(
+                out=w_codes[:].rearrange("q g n -> q (g n)").bitcast(FP8X4),
+                scales=w_scales[:].rearrange("q g n -> q (g n)"),
+                in_=w_grouped[:].rearrange("q g n t -> q (g n t)"),
+            )
+
+        def transpose_pairs(rows, grouped, passes):
+            words = rows[:].bitcast(F32)
+            grouped_words = grouped[:].bitcast(F32).rearrange("q (g m u) -> q g m u", g=passes, u=2)
+            for bank in range(passes // PASSES_PER_BANK):
+                flipped = flip_psum.tile([P, 2 * PASSES_PER_BANK, P], F32)
+                for j in range(2 * PASSES_PER_BANK):
+                    block = bank * 2 * PASSES_PER_BANK + j
+                    nc.tensor.transpose(
+                        flipped[:, j, :], words[:, block * P : (block + 1) * P], identity[:]
+                    )
+                copy_part(
+                    bank,
+                    grouped_words[:, bank * PASSES_PER_BANK : (bank + 1) * PASSES_PER_BANK, :, :],
+                    flipped[:].rearrange("q (g u) m -> q g m u", u=2),
+                )
+
+        def quantise_rows(grouped, passes, pool):
+            codes = pool.tile([P, passes, P], U32, align_bytes=64, name="codes%d" % passes)
+            scales = pool.tile([P, passes, P], U8, align_bytes=64, name="scales%d" % passes)
+            nc.vector.quantize_mx(
+                out=codes[:].rearrange("q g m -> q (g m)").bitcast(FP8X4),
+                scales=scales[:].rearrange("q g m -> q (g m)"),
+                in_=grouped[:],
+            )
+            return codes, scales
+
+        a_grouped_of = {}
+        a_quantised_of = {}
+        t5_rows_of = {}
+        t_rows_of = {}
+        t_grouped_of = {}
+        t_quantised_of = {}
+
+        def transpose_a(i):
+            a_grouped = stage.tile([P, NODES], BF16, align_bytes=64)
+            transpose_pairs(a_rows_of[i], a_grouped, NODE_PASSES)
+            a_grouped_of[i] = a_grouped
+
+        def quantise_a(i):
+            a_quantised_of[i] = quantise_rows(a_grouped_of[i], NODE_PASSES, ring)
+
+        def first_matmul(i):
+            a_codes, a_scales = a_quantised_of[i]
+            t5_rows = ring.tile([P, FEATS], F32)
+            for half in range(HALVES):
+                cols = slice(half * BANK, (half + 1) * BANK)
+                t5_acc = t5_psum.tile([P, BANK], F32)
+                for g in range(NODE_PASSES):
+                    nc.tensor.matmul_mx(
+                        out=t5_acc[:],
+                        lhsT=a_codes[:, g, :].bitcast(FP8X4),
+                        lhsT_scale=a_scales[:, g, :],
+                        rhs=h_codes[:, g, cols].bitcast(FP8X4),
+                        rhs_scale=h_scales[:, g, cols],
+                        start=(g == 0),
+                        stop=(g == NODE_PASSES - 1),
+                    )
+                nc.scalar.copy(out=t5_rows[:, cols], in_=t5_acc[:])
+            nc.sync.dma_start(out=out_0[i * P : (i + 1) * P, :], in_=t5_rows[:])
+            t5_rows_of[i] = t5_rows
+
+        def round_t(i):
+            t_rows = stage.tile([P, FEATS], BF16)
+            nc.vector.tensor_copy(out=t_rows[:], in_=t5_rows_of[i][:])
+            t_rows_of[i] = t_rows
+
+        def transpose_t(i):
+            t_grouped = stage.tile([P, FEATS], BF16, align_bytes=64)
+            transpose_pairs(t_rows_of[i], t_grouped, FEAT_PASSES)
+            t_grouped_of[i] = t_grouped
+
+        def quantise_t(i):
+            t_quantised_of[i] = quantise_rows(t_grouped_of[i], FEAT_PASSES, stage)
+
+        def second_matmul(i):
+            t_codes, t_scales = t_quantised_of[i]
+            a5_acc = a5_psum.tile([P, OUTS], F32)
+            for g in range(FEAT_PASSES):
+                nc.tensor.matmul_mx(
+                    out=a5_acc[:],
+                    lhsT=t_codes[:, g, :].bitcast(FP8X4),
+                    lhsT_scale=t_scales[:, g, :],
+                    rhs=w_codes[:, g, :].bitcast(FP8X4),
+                    rhs_scale=w_scales[:, g, :],
+                    start=(g == 0),
+                    stop=(g == FEAT_PASSES - 1),
+                )
+            a5_rows = ring.tile([P, OUTS], F32)
+            z_rows = ring.tile([P, OUTS], F32)
+            nc.scalar.copy(out=a5_rows[:], in_=a5_acc[:])
+            nc.scalar.activation(
+                out=z_rows[:], in_=a5_acc[:], func=mybir.ActivationFunctionType.Sigmoid
+            )
+            nc.sync.dma_start(out=out_1[i * P : (i + 1) * P, :], in_=a5_rows[:])
+            nc.sync.dma_start(out=out_2[i * P : (i + 1) * P, :], in_=z_rows[:])
+
+        def is_tile(i):
+            return 0 <= i < ROW_TILES
+
+        transpose_a(0)
+        quantise_a(0)
+        for g in range(NODE_PASSES):
+            quantise_h(g)
+        first_matmul(0)
+        transpose_a(1)
+        quantise_a(1)
+        quantise_w()
+
+        for s in range(1, ROW_TILES + 2):
+            if is_tile(s + 1):
+                transpose_a(s + 1)
+            if is_tile(s - 2):
+                transpose_t(s - 2)
+            if is_tile(s - 1):
+                round_t(s - 1)
+            if is_tile(s - 2):
+                quantise_t(s - 2)
+            if is_tile(s + 1):
+                quantise_a(s + 1)
+            if is_tile(s):
+                first_matmul(s)
+            if is_tile(s - 2):
+                second_matmul(s - 2)

@@ -13,6 +13,7 @@ P = 128
 PACK = 4
 K_PASS = P * PACK
 BANK = 512
+PSUM_BANKS = 8
 PASSES_PER_BANK = 2
 
 NODES = 2048
@@ -23,21 +24,22 @@ ROW_TILES = NODES // P
 NODE_PASSES = NODES // K_PASS
 FEAT_PASSES = FEATS // K_PASS
 HALVES = FEATS // BANK
+GROUP = 4
+assert HALVES * GROUP <= PSUM_BANKS and ROW_TILES % GROUP == 0
 
 FLOPS = 2 * NODES * NODES * FEATS + 2 * NODES * FEATS * OUTS
 
 
 def tile_gcn_kron_pb_kernel(tc, h4, A, W4, out_0, out_1, out_2):
     nc = tc.nc
+    groups = [list(range(first, first + GROUP)) for first in range(0, ROW_TILES, GROUP)]
     with ExitStack() as ctx:
         keep = ctx.enter_context(tc.tile_pool(name="keep", bufs=1))
         a_in = ctx.enter_context(tc.tile_pool(name="a_in", bufs=ROW_TILES))
         h_in = ctx.enter_context(tc.tile_pool(name="h_in", bufs=NODE_PASSES))
         stage = ctx.enter_context(tc.tile_pool(name="stage", bufs=2))
-        ring = ctx.enter_context(tc.tile_pool(name="ring", bufs=3))
-        flip_psum = ctx.enter_context(tc.psum_pool(name="flip_psum", bufs=4))
-        t5_psum = ctx.enter_context(tc.psum_pool(name="t5_psum", bufs=3))
-        a5_psum = ctx.enter_context(tc.psum_pool(name="a5_psum", bufs=1))
+        per_tile = ctx.enter_context(tc.tile_pool(name="per_tile", bufs=GROUP))
+        psum = ctx.enter_context(tc.psum_pool(name="psum", bufs=PSUM_BANKS))
         ctx.enter_context(tc.manual_schedule())
 
         identity = keep.tile([P, P], F32)
@@ -59,17 +61,18 @@ def tile_gcn_kron_pb_kernel(tc, h4, A, W4, out_0, out_1, out_2):
             )
             h_rows_of[g] = h_rows
 
-        load_a(0)
+        for i in groups[0]:
+            load_a(i)
         for g in range(NODE_PASSES):
             load_h(g)
-        load_a(1)
         w_rows = keep.tile([P, FEAT_PASSES, PACK, OUTS], BF16)
         nc.sync.dma_start(
             out=w_rows[:].rearrange("q g (u e) n -> q (g u) e n", e=2),
             in_=W4.rearrange("(gu q e) n -> q gu e n", q=P, e=2),
         )
-        for i in range(2, ROW_TILES):
-            load_a(i)
+        for group in groups[1:]:
+            for i in group:
+                load_a(i)
 
         h_codes = keep.tile([P, NODE_PASSES, FEATS], U32, align_bytes=64)
         h_scales = keep.tile([P, NODE_PASSES, FEATS], U8, align_bytes=64)
@@ -109,25 +112,25 @@ def tile_gcn_kron_pb_kernel(tc, h4, A, W4, out_0, out_1, out_2):
                 in_=w_grouped[:].rearrange("q g n t -> q (g n t)"),
             )
 
-        def transpose_pairs(rows, grouped, passes):
+        def transpose_pairs(rows, grouped, passes, first_part):
             words = rows[:].bitcast(F32)
             grouped_words = grouped[:].bitcast(F32).rearrange("q (g m u) -> q g m u", g=passes, u=2)
             for bank in range(passes // PASSES_PER_BANK):
-                flipped = flip_psum.tile([P, 2 * PASSES_PER_BANK, P], F32)
+                flipped = psum.tile([P, 2 * PASSES_PER_BANK, P], F32, tag="bank")
                 for j in range(2 * PASSES_PER_BANK):
                     block = bank * 2 * PASSES_PER_BANK + j
                     nc.tensor.transpose(
                         flipped[:, j, :], words[:, block * P : (block + 1) * P], identity[:]
                     )
                 copy_part(
-                    bank,
+                    first_part + bank,
                     grouped_words[:, bank * PASSES_PER_BANK : (bank + 1) * PASSES_PER_BANK, :, :],
                     flipped[:].rearrange("q (g u) m -> q g m u", u=2),
                 )
 
-        def quantise_rows(grouped, passes, pool):
-            codes = pool.tile([P, passes, P], U32, align_bytes=64, name="codes%d" % passes)
-            scales = pool.tile([P, passes, P], U8, align_bytes=64, name="scales%d" % passes)
+        def quantise_rows(grouped, passes):
+            codes = per_tile.tile([P, passes, P], U32, align_bytes=64, name="codes%d" % passes)
+            scales = per_tile.tile([P, passes, P], U8, align_bytes=64, name="scales%d" % passes)
             nc.vector.quantize_mx(
                 out=codes[:].rearrange("q g m -> q (g m)").bitcast(FP8X4),
                 scales=scales[:].rearrange("q g m -> q (g m)"),
@@ -135,57 +138,52 @@ def tile_gcn_kron_pb_kernel(tc, h4, A, W4, out_0, out_1, out_2):
             )
             return codes, scales
 
-        a_grouped_of = {}
         a_quantised_of = {}
         t5_rows_of = {}
         t_rows_of = {}
-        t_grouped_of = {}
         t_quantised_of = {}
 
-        def transpose_a(i):
-            a_grouped = stage.tile([P, NODES], BF16, align_bytes=64)
-            transpose_pairs(a_rows_of[i], a_grouped, NODE_PASSES)
-            a_grouped_of[i] = a_grouped
+        def prepare(tiles, rows_of, quantised_of, passes, first_part):
+            waiting = None
+            for i in tiles:
+                grouped = per_tile.tile([P, passes * K_PASS], BF16, align_bytes=64, name="grouped%d" % passes)
+                transpose_pairs(rows_of[i], grouped, passes, first_part)
+                if waiting is not None:
+                    quantised_of[waiting[0]] = quantise_rows(waiting[1], passes)
+                waiting = (i, grouped)
+            quantised_of[waiting[0]] = quantise_rows(waiting[1], passes)
 
-        def quantise_a(i):
-            a_quantised_of[i] = quantise_rows(a_grouped_of[i], NODE_PASSES, ring)
-
-        def first_matmul(i):
-            a_codes, a_scales = a_quantised_of[i]
-            t5_rows = ring.tile([P, FEATS], F32)
-            for half in range(HALVES):
+        def first_matmul(passes_in_order):
+            t5_acc_of = {}
+            for i, half, g in passes_in_order:
                 cols = slice(half * BANK, (half + 1) * BANK)
-                t5_acc = t5_psum.tile([P, BANK], F32)
-                for g in range(NODE_PASSES):
-                    nc.tensor.matmul_mx(
-                        out=t5_acc[:],
-                        lhsT=a_codes[:, g, :].bitcast(FP8X4),
-                        lhsT_scale=a_scales[:, g, :],
-                        rhs=h_codes[:, g, cols].bitcast(FP8X4),
-                        rhs_scale=h_scales[:, g, cols],
-                        start=(g == 0),
-                        stop=(g == NODE_PASSES - 1),
-                    )
-                nc.scalar.copy(out=t5_rows[:, cols], in_=t5_acc[:])
-            nc.sync.dma_start(out=out_0[i * P : (i + 1) * P, :], in_=t5_rows[:])
-            t5_rows_of[i] = t5_rows
-
-        def round_t(i):
-            t_rows = stage.tile([P, FEATS], BF16)
-            nc.vector.tensor_copy(out=t_rows[:], in_=t5_rows_of[i][:])
-            t_rows_of[i] = t_rows
-
-        def transpose_t(i):
-            t_grouped = stage.tile([P, FEATS], BF16, align_bytes=64)
-            transpose_pairs(t_rows_of[i], t_grouped, FEAT_PASSES)
-            t_grouped_of[i] = t_grouped
-
-        def quantise_t(i):
-            t_quantised_of[i] = quantise_rows(t_grouped_of[i], FEAT_PASSES, stage)
+                if g == 0:
+                    t5_acc = psum.tile([P, BANK], F32, tag="bank")
+                    t5_acc_of[(i, half)] = t5_acc
+                if g == 0 and half == 0:
+                    t5_rows = per_tile.tile([P, FEATS], F32)
+                    t5_rows_of[i] = t5_rows
+                a_codes, a_scales = a_quantised_of[i]
+                nc.tensor.matmul_mx(
+                    out=t5_acc_of[(i, half)][:],
+                    lhsT=a_codes[:, g, :].bitcast(FP8X4),
+                    lhsT_scale=a_scales[:, g, :],
+                    rhs=h_codes[:, g, cols].bitcast(FP8X4),
+                    rhs_scale=h_scales[:, g, cols],
+                    start=(g == 0),
+                    stop=(g == NODE_PASSES - 1),
+                )
+                if g == NODE_PASSES - 1:
+                    nc.scalar.copy(out=t5_rows_of[i][:, cols], in_=t5_acc_of[(i, half)][:])
+                if g == NODE_PASSES - 1 and half == HALVES - 1:
+                    nc.sync.dma_start(out=out_0[i * P : (i + 1) * P, :], in_=t5_rows_of[i][:])
+                    t_rows = per_tile.tile([P, FEATS], BF16)
+                    nc.vector.tensor_copy(out=t_rows[:], in_=t5_rows_of[i][:])
+                    t_rows_of[i] = t_rows
 
         def second_matmul(i):
             t_codes, t_scales = t_quantised_of[i]
-            a5_acc = a5_psum.tile([P, OUTS], F32)
+            a5_acc = psum.tile([P, OUTS], F32, tag="bank")
             for g in range(FEAT_PASSES):
                 nc.tensor.matmul_mx(
                     out=a5_acc[:],
@@ -196,39 +194,32 @@ def tile_gcn_kron_pb_kernel(tc, h4, A, W4, out_0, out_1, out_2):
                     start=(g == 0),
                     stop=(g == FEAT_PASSES - 1),
                 )
-            a5_rows = ring.tile([P, OUTS], F32)
-            z_rows = ring.tile([P, OUTS], F32)
-            nc.scalar.copy(out=a5_rows[:], in_=a5_acc[:])
+            a5_rows = per_tile.tile([P, OUTS], F32)
+            z_rows = per_tile.tile([P, OUTS], F32)
+            nc.vector.tensor_copy(out=a5_rows[:], in_=a5_acc[:])
             nc.scalar.activation(
                 out=z_rows[:], in_=a5_acc[:], func=mybir.ActivationFunctionType.Sigmoid
             )
             nc.sync.dma_start(out=out_1[i * P : (i + 1) * P, :], in_=a5_rows[:])
             nc.sync.dma_start(out=out_2[i * P : (i + 1) * P, :], in_=z_rows[:])
 
-        def is_tile(i):
-            return 0 <= i < ROW_TILES
+        all_halves = range(HALVES)
+        all_passes = range(NODE_PASSES)
 
-        transpose_a(0)
-        quantise_a(0)
-        for g in range(NODE_PASSES):
+        prepare(groups[0], a_rows_of, a_quantised_of, NODE_PASSES, 0)
+        for g in all_passes:
             quantise_h(g)
-        first_matmul(0)
-        transpose_a(1)
-        quantise_a(1)
-        quantise_w()
+        first_matmul([(i, half, g) for g in all_passes for half in all_halves for i in groups[0]])
 
-        for s in range(1, ROW_TILES + 2):
-            if is_tile(s + 1):
-                transpose_a(s + 1)
-            if is_tile(s - 2):
-                transpose_t(s - 2)
-            if is_tile(s - 1):
-                round_t(s - 1)
-            if is_tile(s - 2):
-                quantise_t(s - 2)
-            if is_tile(s + 1):
-                quantise_a(s + 1)
-            if is_tile(s):
-                first_matmul(s)
-            if is_tile(s - 2):
-                second_matmul(s - 2)
+        for n in range(1, len(groups)):
+            prepare(groups[n], a_rows_of, a_quantised_of, NODE_PASSES, 0)
+            prepare(groups[n - 1], t_rows_of, t_quantised_of, FEAT_PASSES, 1)
+            if n == 1:
+                quantise_w()
+            first_matmul([(i, half, g) for i in groups[n] for half in all_halves for g in all_passes])
+            for i in groups[n - 1]:
+                second_matmul(i)
+
+        prepare(groups[-1], t_rows_of, t_quantised_of, FEAT_PASSES, 1)
+        for i in groups[-1]:
+            second_matmul(i)

@@ -24,21 +24,24 @@ ROW_TILES = NODES // P
 NODE_PASSES = NODES // K_PASS
 FEAT_PASSES = FEATS // K_PASS
 HALVES = FEATS // BANK
-GROUP = 4
-assert HALVES * GROUP <= PSUM_BANKS and ROW_TILES % GROUP == 0
+FIRST_GROUP = PSUM_BANKS // HALVES
+GROUP = 2
+assert (ROW_TILES - FIRST_GROUP) % GROUP == 0 and GROUP <= FIRST_GROUP
 
 FLOPS = 2 * NODES * NODES * FEATS + 2 * NODES * FEATS * OUTS
 
 
 def tile_gcn_kron_pb_kernel(tc, h4, A, W4, out_0, out_1, out_2):
     nc = tc.nc
-    groups = [list(range(first, first + GROUP)) for first in range(0, ROW_TILES, GROUP)]
+    groups = [list(range(FIRST_GROUP))] + [
+        list(range(first, first + GROUP)) for first in range(FIRST_GROUP, ROW_TILES, GROUP)
+    ]
     with ExitStack() as ctx:
         keep = ctx.enter_context(tc.tile_pool(name="keep", bufs=1))
         a_in = ctx.enter_context(tc.tile_pool(name="a_in", bufs=ROW_TILES))
         h_in = ctx.enter_context(tc.tile_pool(name="h_in", bufs=NODE_PASSES))
         stage = ctx.enter_context(tc.tile_pool(name="stage", bufs=2))
-        per_tile = ctx.enter_context(tc.tile_pool(name="per_tile", bufs=GROUP))
+        per_tile = ctx.enter_context(tc.tile_pool(name="per_tile", bufs=FIRST_GROUP))
         psum = ctx.enter_context(tc.psum_pool(name="psum", bufs=PSUM_BANKS))
         ctx.enter_context(tc.manual_schedule())
 

@@ -24,24 +24,28 @@ ROW_TILES = NODES // P
 NODE_PASSES = NODES // K_PASS
 FEAT_PASSES = FEATS // K_PASS
 HALVES = FEATS // BANK
-FIRST_GROUP = PSUM_BANKS // HALVES
-GROUP = 2
-assert (ROW_TILES - FIRST_GROUP) % GROUP == 0 and GROUP <= FIRST_GROUP
+PAIR = 2
+GROUP_PAIRS = 2
+assert PAIR * OUTS == BANK and GROUP_PAIRS * PAIR * HALVES == PSUM_BANKS
+A_BUFFERS = 8
 
 FLOPS = 2 * NODES * NODES * FEATS + 2 * NODES * FEATS * OUTS
 
 
+def tiles_of(pairs):
+    return [PAIR * p + j for p in pairs for j in range(PAIR)]
+
+
 def tile_gcn_kron_pb_kernel(tc, h4, A, W4, out_0, out_1, out_2):
     nc = tc.nc
-    groups = [list(range(FIRST_GROUP))] + [
-        list(range(first, first + GROUP)) for first in range(FIRST_GROUP, ROW_TILES, GROUP)
-    ]
+    all_pairs = list(range(ROW_TILES // PAIR))
+    groups = [all_pairs[first : first + GROUP_PAIRS] for first in range(0, len(all_pairs), GROUP_PAIRS)]
     with ExitStack() as ctx:
         keep = ctx.enter_context(tc.tile_pool(name="keep", bufs=1))
-        a_in = ctx.enter_context(tc.tile_pool(name="a_in", bufs=ROW_TILES))
+        a_in = ctx.enter_context(tc.tile_pool(name="a_in", bufs=A_BUFFERS))
         h_in = ctx.enter_context(tc.tile_pool(name="h_in", bufs=NODE_PASSES))
-        stage = ctx.enter_context(tc.tile_pool(name="stage", bufs=2))
-        per_tile = ctx.enter_context(tc.tile_pool(name="per_tile", bufs=FIRST_GROUP))
+        two = ctx.enter_context(tc.tile_pool(name="two", bufs=2))
+        four = ctx.enter_context(tc.tile_pool(name="four", bufs=4))
         psum = ctx.enter_context(tc.psum_pool(name="psum", bufs=PSUM_BANKS))
         ctx.enter_context(tc.manual_schedule())
 
@@ -64,7 +68,7 @@ def tile_gcn_kron_pb_kernel(tc, h4, A, W4, out_0, out_1, out_2):
             )
             h_rows_of[g] = h_rows
 
-        for i in groups[0]:
+        for i in tiles_of(groups[0]):
             load_a(i)
         for g in range(NODE_PASSES):
             load_h(g)
@@ -73,9 +77,8 @@ def tile_gcn_kron_pb_kernel(tc, h4, A, W4, out_0, out_1, out_2):
             out=w_rows[:].rearrange("q g (u e) n -> q (g u) e n", e=2),
             in_=W4.rearrange("(gu q e) n -> q gu e n", q=P, e=2),
         )
-        for group in groups[1:]:
-            for i in group:
-                load_a(i)
+        for i in tiles_of(groups[1]):
+            load_a(i)
 
         h_codes = keep.tile([P, NODE_PASSES, FEATS], U32, align_bytes=64)
         h_scales = keep.tile([P, NODE_PASSES, FEATS], U8, align_bytes=64)
@@ -89,7 +92,7 @@ def tile_gcn_kron_pb_kernel(tc, h4, A, W4, out_0, out_1, out_2):
                 nc.scalar.copy(out=out, in_=in_)
 
         def quantise_h(g):
-            h_grouped = stage.tile([P, FEATS, PACK], BF16, align_bytes=64)
+            h_grouped = two.tile([P, FEATS, PACK], BF16, align_bytes=64)
             for half in range(HALVES):
                 cols = slice(half * BANK, (half + 1) * BANK)
                 copy_part(
@@ -116,8 +119,8 @@ def tile_gcn_kron_pb_kernel(tc, h4, A, W4, out_0, out_1, out_2):
             )
 
         def transpose_pairs(rows, grouped, passes, first_part):
-            words = rows[:].bitcast(F32)
-            grouped_words = grouped[:].bitcast(F32).rearrange("q (g m u) -> q g m u", g=passes, u=2)
+            words = rows.bitcast(F32)
+            grouped_words = grouped.bitcast(F32).rearrange("q (g m u) -> q g m u", g=passes, u=2)
             for bank in range(passes // PASSES_PER_BANK):
                 flipped = psum.tile([P, 2 * PASSES_PER_BANK, P], F32, tag="bank")
                 for j in range(2 * PASSES_PER_BANK):
@@ -131,30 +134,32 @@ def tile_gcn_kron_pb_kernel(tc, h4, A, W4, out_0, out_1, out_2):
                     flipped[:].rearrange("q (g u) m -> q g m u", u=2),
                 )
 
-        def quantise_rows(grouped, passes):
-            codes = per_tile.tile([P, passes, P], U32, align_bytes=64, name="codes%d" % passes)
-            scales = per_tile.tile([P, passes, P], U8, align_bytes=64, name="scales%d" % passes)
-            nc.vector.quantize_mx(
-                out=codes[:].rearrange("q g m -> q (g m)").bitcast(FP8X4),
-                scales=scales[:].rearrange("q g m -> q (g m)"),
-                in_=grouped[:],
-            )
-            return codes, scales
-
         a_quantised_of = {}
         t5_rows_of = {}
         t_rows_of = {}
         t_quantised_of = {}
 
-        def prepare(tiles, rows_of, quantised_of, passes, first_part):
+        def quantise_a(i, a_grouped):
+            a_codes = four.tile([P, NODE_PASSES, P], U32, align_bytes=64)
+            a_scales = four.tile([P, NODE_PASSES, P], U8, align_bytes=64)
+            nc.vector.quantize_mx(
+                out=a_codes[:].rearrange("q g m -> q (g m)").bitcast(FP8X4),
+                scales=a_scales[:].rearrange("q g m -> q (g m)"),
+                in_=a_grouped[:],
+            )
+            a_quantised_of[i] = (a_codes, a_scales)
+
+        def prepare_a(tiles):
             waiting = None
             for i in tiles:
-                grouped = per_tile.tile([P, passes * K_PASS], BF16, align_bytes=64, name="grouped%d" % passes)
-                transpose_pairs(rows_of[i], grouped, passes, first_part)
+                a_grouped = four.tile([P, NODES], BF16, align_bytes=64)
+                transpose_pairs(a_rows_of[i][:], a_grouped[:], NODE_PASSES, 0)
+                if i + A_BUFFERS < ROW_TILES:
+                    load_a(i + A_BUFFERS)
                 if waiting is not None:
-                    quantised_of[waiting[0]] = quantise_rows(waiting[1], passes)
-                waiting = (i, grouped)
-            quantised_of[waiting[0]] = quantise_rows(waiting[1], passes)
+                    quantise_a(waiting[0], waiting[1])
+                waiting = (i, a_grouped)
+            quantise_a(waiting[0], waiting[1])
 
         def first_matmul(passes_in_order):
             t5_acc_of = {}
@@ -163,9 +168,9 @@ def tile_gcn_kron_pb_kernel(tc, h4, A, W4, out_0, out_1, out_2):
                 if g == 0:
                     t5_acc = psum.tile([P, BANK], F32, tag="bank")
                     t5_acc_of[(i, half)] = t5_acc
-                if g == 0 and half == 0:
-                    t5_rows = per_tile.tile([P, FEATS], F32)
-                    t5_rows_of[i] = t5_rows
+                if g == 0 and half == 0 and i % PAIR == 0:
+                    t5_rows = four.tile([P, PAIR, FEATS], F32)
+                    t5_rows_of[i // PAIR] = t5_rows
                 a_codes, a_scales = a_quantised_of[i]
                 nc.tensor.matmul_mx(
                     out=t5_acc_of[(i, half)][:],
@@ -177,52 +182,91 @@ def tile_gcn_kron_pb_kernel(tc, h4, A, W4, out_0, out_1, out_2):
                     stop=(g == NODE_PASSES - 1),
                 )
                 if g == NODE_PASSES - 1:
-                    nc.scalar.copy(out=t5_rows_of[i][:, cols], in_=t5_acc_of[(i, half)][:])
+                    copy_part(half, t5_rows_of[i // PAIR][:, i % PAIR, cols], t5_acc_of[(i, half)][:])
                 if g == NODE_PASSES - 1 and half == HALVES - 1:
-                    nc.sync.dma_start(out=out_0[i * P : (i + 1) * P, :], in_=t5_rows_of[i][:])
-                    t_rows = per_tile.tile([P, FEATS], BF16)
-                    nc.vector.tensor_copy(out=t_rows[:], in_=t5_rows_of[i][:])
-                    t_rows_of[i] = t_rows
+                    nc.sync.dma_start(
+                        out=out_0[i * P : (i + 1) * P, :], in_=t5_rows_of[i // PAIR][:, i % PAIR, :]
+                    )
 
-        def second_matmul(i):
-            t_codes, t_scales = t_quantised_of[i]
-            a5_acc = psum.tile([P, OUTS], F32, tag="bank")
-            for g in range(FEAT_PASSES):
-                nc.tensor.matmul_mx(
-                    out=a5_acc[:],
-                    lhsT=t_codes[:, g, :].bitcast(FP8X4),
-                    lhsT_scale=t_scales[:, g, :],
-                    rhs=w_codes[:, g, :].bitcast(FP8X4),
-                    rhs_scale=w_scales[:, g, :],
-                    start=(g == 0),
-                    stop=(g == FEAT_PASSES - 1),
-                )
-            a5_rows = per_tile.tile([P, OUTS], F32)
-            z_rows = per_tile.tile([P, OUTS], F32)
-            nc.vector.tensor_copy(out=a5_rows[:], in_=a5_acc[:])
+        def round_t(p):
+            t_rows = four.tile([P, PAIR, FEATS], BF16)
+            nc.vector.tensor_copy(out=t_rows[:], in_=t5_rows_of[p][:])
+            t_rows_of[p] = t_rows
+
+        def quantise_t(p, t_grouped):
+            t_codes = four.tile([P, PAIR, FEAT_PASSES, P], U32, align_bytes=64)
+            t_scales = four.tile([P, PAIR, FEAT_PASSES, P], U8, align_bytes=64)
+            nc.vector.quantize_mx(
+                out=t_codes[:].rearrange("q j g m -> q (j g m)").bitcast(FP8X4),
+                scales=t_scales[:].rearrange("q j g m -> q (j g m)"),
+                in_=t_grouped[:].rearrange("q j k -> q (j k)"),
+            )
+            t_quantised_of[p] = (t_codes, t_scales)
+
+        def prepare_t(pairs):
+            waiting = None
+            for p in pairs:
+                t_grouped = two.tile([P, PAIR, FEATS], BF16, align_bytes=64)
+                for j in range(PAIR):
+                    transpose_pairs(t_rows_of[p][:, j, :], t_grouped[:, j, :], FEAT_PASSES, 1)
+                if waiting is not None:
+                    quantise_t(waiting[0], waiting[1])
+                waiting = (p, t_grouped)
+            quantise_t(waiting[0], waiting[1])
+
+        def second_matmul(p):
+            t_codes, t_scales = t_quantised_of[p]
+            a5_acc = psum.tile([P, PAIR, OUTS], F32, tag="bank")
+            for j in range(PAIR):
+                for g in range(FEAT_PASSES):
+                    nc.tensor.matmul_mx(
+                        out=a5_acc[:, j, :],
+                        lhsT=t_codes[:, j, g, :].bitcast(FP8X4),
+                        lhsT_scale=t_scales[:, j, g, :],
+                        rhs=w_codes[:, g, :].bitcast(FP8X4),
+                        rhs_scale=w_scales[:, g, :],
+                        start=(g == 0),
+                        stop=(g == FEAT_PASSES - 1),
+                    )
+            a5_rows = four.tile([P, PAIR, OUTS], F32)
+            z_rows = four.tile([P, PAIR, OUTS], F32)
+            nc.scalar.copy(out=a5_rows[:], in_=a5_acc[:])
             nc.scalar.activation(
                 out=z_rows[:], in_=a5_acc[:], func=mybir.ActivationFunctionType.Sigmoid
             )
-            nc.sync.dma_start(out=out_1[i * P : (i + 1) * P, :], in_=a5_rows[:])
-            nc.sync.dma_start(out=out_2[i * P : (i + 1) * P, :], in_=z_rows[:])
+            rows = slice(p * PAIR * P, (p + 1) * PAIR * P)
+            nc.sync.dma_start(out=out_1[rows, :].rearrange("(j m) n -> m j n", j=PAIR), in_=a5_rows[:])
+            nc.sync.dma_start(out=out_2[rows, :].rearrange("(j m) n -> m j n", j=PAIR), in_=z_rows[:])
 
         all_halves = range(HALVES)
         all_passes = range(NODE_PASSES)
 
-        prepare(groups[0], a_rows_of, a_quantised_of, NODE_PASSES, 0)
+        def tile_by_tile(pairs):
+            return [(i, half, g) for i in tiles_of(pairs) for half in all_halves for g in all_passes]
+
+        prepare_a(tiles_of(groups[0]))
         for g in all_passes:
             quantise_h(g)
-        first_matmul([(i, half, g) for g in all_passes for half in all_halves for i in groups[0]])
+        first_matmul(
+            [(i, half, g) for g in all_passes for half in all_halves for i in tiles_of(groups[0])]
+        )
 
         for n in range(1, len(groups)):
-            prepare(groups[n], a_rows_of, a_quantised_of, NODE_PASSES, 0)
-            prepare(groups[n - 1], t_rows_of, t_quantised_of, FEAT_PASSES, 1)
+            prepare_a(tiles_of(groups[n]))
+            if n >= 2:
+                prepare_t(groups[n - 2])
+            for p in groups[n - 1]:
+                round_t(p)
             if n == 1:
                 quantise_w()
-            first_matmul([(i, half, g) for i in groups[n] for half in all_halves for g in all_passes])
-            for i in groups[n - 1]:
-                second_matmul(i)
+            first_matmul(tile_by_tile(groups[n][:1]))
+            if n >= 2:
+                for p in groups[n - 2]:
+                    second_matmul(p)
+            first_matmul(tile_by_tile(groups[n][1:]))
 
-        prepare(groups[-1], t_rows_of, t_quantised_of, FEAT_PASSES, 1)
-        for i in groups[-1]:
-            second_matmul(i)
+        for p in groups[-1]:
+            round_t(p)
+        prepare_t(groups[-2] + groups[-1])
+        for p in groups[-2] + groups[-1]:
+            second_matmul(p)

@@ -26,7 +26,8 @@ FEAT_PASSES = FEATS // K_PASS
 HALVES = FEATS // BANK
 PAIR = 2
 GROUP_PAIRS = 2
-assert PAIR * OUTS == BANK and GROUP_PAIRS * PAIR * HALVES == PSUM_BANKS
+assert PAIR * OUTS == BANK
+H_SPLIT = 512
 A_BUFFERS = 8
 
 FLOPS = 2 * NODES * NODES * FEATS + 2 * NODES * FEATS * OUTS
@@ -45,8 +46,11 @@ def tile_gcn_kron_pb_kernel(tc, h4, A, W4, out_0, out_1, out_2):
         a_in = ctx.enter_context(tc.tile_pool(name="a_in", bufs=A_BUFFERS))
         h_in = ctx.enter_context(tc.tile_pool(name="h_in", bufs=NODE_PASSES))
         two = ctx.enter_context(tc.tile_pool(name="two", bufs=2))
+        three = ctx.enter_context(tc.tile_pool(name="three", bufs=3))
         four = ctx.enter_context(tc.tile_pool(name="four", bufs=4))
-        psum = ctx.enter_context(tc.psum_pool(name="psum", bufs=PSUM_BANKS))
+        five = ctx.enter_context(tc.tile_pool(name="five", bufs=5))
+        six = ctx.enter_context(tc.tile_pool(name="six", bufs=6))
+        psum = ctx.enter_context(tc.psum_pool(name="psum", bufs=8))
         ctx.enter_context(tc.manual_schedule())
 
         identity = keep.tile([P, P], F32)
@@ -55,9 +59,13 @@ def tile_gcn_kron_pb_kernel(tc, h4, A, W4, out_0, out_1, out_2):
         a_rows_of = {}
         h_rows_of = {}
 
+        def rows_of(x, i):
+            first = (i // PAIR) * PAIR * P
+            return x[first : first + PAIR * P, :].rearrange("(m j) n -> m j n", j=PAIR)[:, i % PAIR, :]
+
         def load_a(i):
             a_rows = a_in.tile([P, NODES], BF16)
-            nc.sync.dma_start(out=a_rows[:], in_=A[i * P : (i + 1) * P, :])
+            nc.sync.dma_start(out=a_rows[:], in_=rows_of(A, i))
             a_rows_of[i] = a_rows
 
         def load_h(g):
@@ -68,57 +76,49 @@ def tile_gcn_kron_pb_kernel(tc, h4, A, W4, out_0, out_1, out_2):
             )
             h_rows_of[g] = h_rows
 
-        for i in tiles_of(groups[0]):
-            load_a(i)
-        for g in range(NODE_PASSES):
-            load_h(g)
-        w_rows = keep.tile([P, FEAT_PASSES, PACK, OUTS], BF16)
-        nc.sync.dma_start(
-            out=w_rows[:].rearrange("q g (u e) n -> q (g u) e n", e=2),
-            in_=W4.rearrange("(gu q e) n -> q gu e n", q=P, e=2),
-        )
-        for i in tiles_of(groups[1]):
-            load_a(i)
-
         h_codes = keep.tile([P, NODE_PASSES, FEATS], U32, align_bytes=64)
         h_scales = keep.tile([P, NODE_PASSES, FEATS], U8, align_bytes=64)
         w_codes = keep.tile([P, FEAT_PASSES, OUTS], U32, align_bytes=64)
         w_scales = keep.tile([P, FEAT_PASSES, OUTS], U8, align_bytes=64)
 
-        def copy_part(part, out, in_):
-            if part == 0:
+        def copy_on(engine, out, in_):
+            if engine == "vector":
                 nc.vector.tensor_copy(out=out, in_=in_)
             else:
                 nc.scalar.copy(out=out, in_=in_)
 
-        def quantise_h(g):
-            h_grouped = two.tile([P, FEATS, PACK], BF16, align_bytes=64)
-            for half in range(HALVES):
-                cols = slice(half * BANK, (half + 1) * BANK)
-                copy_part(
-                    half,
-                    h_grouped[:, cols, :].rearrange("q (c i) t -> q c t i", i=4),
-                    h_rows_of[g][:, :, cols].rearrange("q t (c i) -> q c t i", i=4),
-                )
-            for half in range(HALVES):
-                cols = slice(half * BANK, (half + 1) * BANK)
-                nc.vector.quantize_mx(
-                    out=h_codes[:, g, cols].bitcast(FP8X4),
-                    scales=h_scales[:, g, cols],
-                    in_=h_grouped[:, cols, :].rearrange("q c t -> q (c t)"),
-                )
+        h_grouped_of = {}
+
+        def group_h(g, engine, first, last):
+            if g not in h_grouped_of:
+                h_grouped = two.tile([P, FEATS, PACK], BF16, align_bytes=64)
+                h_grouped_of[g] = h_grouped
+            copy_on(
+                engine,
+                h_grouped_of[g][:, first:last, :].rearrange("q (c i) t -> q c t i", i=4),
+                h_rows_of[g][:, :, first:last].rearrange("q t (c i) -> q c t i", i=4),
+            )
+
+        def quantise_h(g, first, last):
+            nc.vector.quantize_mx(
+                out=h_codes[:, g, first:last].bitcast(FP8X4),
+                scales=h_scales[:, g, first:last],
+                in_=h_grouped_of[g][:, first:last, :].rearrange("q c t -> q (c t)"),
+            )
 
         def quantise_w():
-            w_grouped = keep.tile([P, FEAT_PASSES, OUTS, PACK], BF16, align_bytes=64)
+            w_grouped = five.tile([P, FEAT_PASSES, OUTS, PACK], BF16, align_bytes=64, tag="row_tile")
             for g in range(FEAT_PASSES):
-                copy_part(g, w_grouped[:, g, :, :], w_rows[:, g, :, :].rearrange("q t n -> q n t"))
+                nc.vector.tensor_copy(
+                    out=w_grouped[:, g, :, :], in_=w_rows[:, g, :, :].rearrange("q t n -> q n t")
+                )
             nc.vector.quantize_mx(
                 out=w_codes[:].rearrange("q g n -> q (g n)").bitcast(FP8X4),
                 scales=w_scales[:].rearrange("q g n -> q (g n)"),
                 in_=w_grouped[:].rearrange("q g n t -> q (g n t)"),
             )
 
-        def transpose_pairs(rows, grouped, passes, first_part):
+        def transpose_pairs(rows, grouped, passes, engines):
             words = rows.bitcast(F32)
             grouped_words = grouped.bitcast(F32).rearrange("q (g m u) -> q g m u", g=passes, u=2)
             for bank in range(passes // PASSES_PER_BANK):
@@ -128,8 +128,8 @@ def tile_gcn_kron_pb_kernel(tc, h4, A, W4, out_0, out_1, out_2):
                     nc.tensor.transpose(
                         flipped[:, j, :], words[:, block * P : (block + 1) * P], identity[:]
                     )
-                copy_part(
-                    first_part + bank,
+                copy_on(
+                    engines[bank],
                     grouped_words[:, bank * PASSES_PER_BANK : (bank + 1) * PASSES_PER_BANK, :, :],
                     flipped[:].rearrange("q (g u) m -> q g m u", u=2),
                 )
@@ -139,36 +139,32 @@ def tile_gcn_kron_pb_kernel(tc, h4, A, W4, out_0, out_1, out_2):
         t_rows_of = {}
         t_quantised_of = {}
 
-        def quantise_a(i, a_grouped):
-            a_codes = four.tile([P, NODE_PASSES, P], U32, align_bytes=64)
-            a_scales = four.tile([P, NODE_PASSES, P], U8, align_bytes=64)
+        a_grouped_of = {}
+
+        def flip_a(i, engines):
+            a_grouped = five.tile([P, NODES], BF16, align_bytes=64, tag="row_tile")
+            a_grouped_of[i] = a_grouped
+            transpose_pairs(a_rows_of[i][:], a_grouped[:], NODE_PASSES, engines)
+
+        def quantise_a(i):
+            a_codes = six.tile([P, NODE_PASSES, P], U32, align_bytes=64)
+            a_scales = six.tile([P, NODE_PASSES, P], U8, align_bytes=64)
             nc.vector.quantize_mx(
                 out=a_codes[:].rearrange("q g m -> q (g m)").bitcast(FP8X4),
                 scales=a_scales[:].rearrange("q g m -> q (g m)"),
-                in_=a_grouped[:],
+                in_=a_grouped_of[i][:],
             )
             a_quantised_of[i] = (a_codes, a_scales)
 
-        def prepare_a(tiles):
-            waiting = None
-            for i in tiles:
-                a_grouped = four.tile([P, NODES], BF16, align_bytes=64)
-                transpose_pairs(a_rows_of[i][:], a_grouped[:], NODE_PASSES, 0)
-                if i + A_BUFFERS < ROW_TILES:
-                    load_a(i + A_BUFFERS)
-                if waiting is not None:
-                    quantise_a(waiting[0], waiting[1])
-                waiting = (i, a_grouped)
-            quantise_a(waiting[0], waiting[1])
+        t5_acc_of = {}
 
-        def first_matmul(passes_in_order):
-            t5_acc_of = {}
+        def first_matmul(passes_in_order, engine_of, round_from_sums=()):
             for i, half, g in passes_in_order:
                 cols = slice(half * BANK, (half + 1) * BANK)
                 if g == 0:
                     t5_acc = psum.tile([P, BANK], F32, tag="bank")
                     t5_acc_of[(i, half)] = t5_acc
-                if g == 0 and half == 0 and i % PAIR == 0:
+                if i // PAIR not in t5_rows_of:
                     t5_rows = four.tile([P, PAIR, FEATS], F32)
                     t5_rows_of[i // PAIR] = t5_rows
                 a_codes, a_scales = a_quantised_of[i]
@@ -181,92 +177,272 @@ def tile_gcn_kron_pb_kernel(tc, h4, A, W4, out_0, out_1, out_2):
                     start=(g == 0),
                     stop=(g == NODE_PASSES - 1),
                 )
+                if g == NODE_PASSES - 1 and i in round_from_sums:
+                    round_t(i // PAIR, half, slice(i % PAIR, i % PAIR + 1), t5_acc_of[(i, half)][:])
                 if g == NODE_PASSES - 1:
-                    copy_part(half, t5_rows_of[i // PAIR][:, i % PAIR, cols], t5_acc_of[(i, half)][:])
-                if g == NODE_PASSES - 1 and half == HALVES - 1:
-                    nc.sync.dma_start(
-                        out=out_0[i * P : (i + 1) * P, :], in_=t5_rows_of[i // PAIR][:, i % PAIR, :]
+                    copy_on(engine_of(i), t5_rows_of[i // PAIR][:, i % PAIR, cols], t5_acc_of[(i, half)][:])
+
+        def store_t5(tiles, half):
+            cols = slice(half * BANK, (half + 1) * BANK)
+            for i in tiles:
+                nc.sync.dma_start(
+                    out=rows_of(out_0, i)[:, cols], in_=t5_rows_of[i // PAIR][:, i % PAIR, cols]
+                )
+
+        def round_t(p, half, tiles_in_pair=slice(0, PAIR), t5=None):
+            cols = slice(half * BANK, (half + 1) * BANK)
+            if p not in t_rows_of:
+                t_rows = four.tile([P, PAIR, FEATS], BF16)
+                t_rows_of[p] = t_rows
+            t_part = t_rows_of[p][:, tiles_in_pair, cols]
+            if t5 is None:
+                nc.vector.tensor_copy(out=t_part, in_=t5_rows_of[p][:, tiles_in_pair, cols])
+            else:
+                nc.vector.tensor_copy(out=t_part.rearrange("q j k -> q (j k)"), in_=t5)
+
+        t_grouped_of = {}
+
+        def flip_t(p, parts, engine):
+            if p not in t_grouped_of:
+                t_grouped = two.tile([P, PAIR, FEATS], BF16, align_bytes=64)
+                t_grouped_of[p] = t_grouped
+            words = t_rows_of[p][:].rearrange("q j k -> q (j k)").bitcast(F32)
+            grouped_words = (
+                t_grouped_of[p][:].rearrange("q j k -> q (j k)").bitcast(F32)
+            ).rearrange("q (s m u) -> q s m u", s=PAIR * FEAT_PASSES, u=2)
+            flipped = psum.tile([P, 2 * PASSES_PER_BANK, P], F32, tag="bank")
+            slots = [j * FEAT_PASSES + half for j, half in parts]
+            for k, slot in enumerate(slots):
+                for u in range(2):
+                    block = 2 * slot + u
+                    nc.tensor.transpose(
+                        flipped[:, 2 * k + u, :], words[:, block * P : (block + 1) * P], identity[:]
                     )
-
-        def round_t(p):
-            t_rows = four.tile([P, PAIR, FEATS], BF16)
-            nc.vector.tensor_copy(out=t_rows[:], in_=t5_rows_of[p][:])
-            t_rows_of[p] = t_rows
-
-        def quantise_t(p, t_grouped):
-            t_codes = four.tile([P, PAIR, FEAT_PASSES, P], U32, align_bytes=64)
-            t_scales = four.tile([P, PAIR, FEAT_PASSES, P], U8, align_bytes=64)
-            nc.vector.quantize_mx(
-                out=t_codes[:].rearrange("q j g m -> q (j g m)").bitcast(FP8X4),
-                scales=t_scales[:].rearrange("q j g m -> q (j g m)"),
-                in_=t_grouped[:].rearrange("q j k -> q (j k)"),
+            step = slots[-1] - slots[0] if len(slots) > 1 else 1
+            copy_on(
+                engine,
+                grouped_words[:, slots[0] : slots[-1] + 1 : step, :, :],
+                flipped[:, 0 : 2 * len(slots), :].rearrange("q (s u) m -> q s m u", u=2),
             )
-            t_quantised_of[p] = (t_codes, t_scales)
 
-        def prepare_t(pairs):
+        def quantise_t(p, first, last):
+            if p not in t_quantised_of:
+                t_codes = three.tile([P, PAIR * FEAT_PASSES, P], U32, align_bytes=64)
+                t_scales = three.tile([P, PAIR * FEAT_PASSES, P], U8, align_bytes=64)
+                t_quantised_of[p] = (t_codes, t_scales)
+            t_codes, t_scales = t_quantised_of[p]
+            nc.vector.quantize_mx(
+                out=t_codes[:, first:last, :].rearrange("q s m -> q (s m)").bitcast(FP8X4),
+                scales=t_scales[:, first:last, :].rearrange("q s m -> q (s m)"),
+                in_=t_grouped_of[p][:].rearrange("q j k -> q (j k)")[:, first * BANK : last * BANK],
+            )
+
+        def prepare_t(pairs, engines, quantise_last=True):
             waiting = None
             for p in pairs:
-                t_grouped = two.tile([P, PAIR, FEATS], BF16, align_bytes=64)
                 for j in range(PAIR):
-                    transpose_pairs(t_rows_of[p][:, j, :], t_grouped[:, j, :], FEAT_PASSES, 1)
+                    flip_t(p, [(j, 0), (j, 1)], engines[j])
                 if waiting is not None:
-                    quantise_t(waiting[0], waiting[1])
-                waiting = (p, t_grouped)
-            quantise_t(waiting[0], waiting[1])
+                    quantise_t(waiting, 0, PAIR * FEAT_PASSES)
+                waiting = p
+            if quantise_last:
+                quantise_t(waiting, 0, PAIR * FEAT_PASSES)
 
-        def second_matmul(p):
+        def second_matmul(p, tiles_in_pair):
             t_codes, t_scales = t_quantised_of[p]
-            a5_acc = psum.tile([P, PAIR, OUTS], F32, tag="bank")
-            for j in range(PAIR):
+            a5_acc = psum.tile([P, len(tiles_in_pair), OUTS], F32, tag="bank")
+            for k, j in enumerate(tiles_in_pair):
                 for g in range(FEAT_PASSES):
+                    slot = j * FEAT_PASSES + g
                     nc.tensor.matmul_mx(
-                        out=a5_acc[:, j, :],
-                        lhsT=t_codes[:, j, g, :].bitcast(FP8X4),
-                        lhsT_scale=t_scales[:, j, g, :],
+                        out=a5_acc[:, k, :],
+                        lhsT=t_codes[:, slot, :].bitcast(FP8X4),
+                        lhsT_scale=t_scales[:, slot, :],
                         rhs=w_codes[:, g, :].bitcast(FP8X4),
                         rhs_scale=w_scales[:, g, :],
                         start=(g == 0),
                         stop=(g == FEAT_PASSES - 1),
                     )
-            a5_rows = four.tile([P, PAIR, OUTS], F32)
-            z_rows = four.tile([P, PAIR, OUTS], F32)
-            nc.scalar.copy(out=a5_rows[:], in_=a5_acc[:])
-            nc.scalar.activation(
-                out=z_rows[:], in_=a5_acc[:], func=mybir.ActivationFunctionType.Sigmoid
-            )
-            rows = slice(p * PAIR * P, (p + 1) * PAIR * P)
-            nc.sync.dma_start(out=out_1[rows, :].rearrange("(j m) n -> m j n", j=PAIR), in_=a5_rows[:])
-            nc.sync.dma_start(out=out_2[rows, :].rearrange("(j m) n -> m j n", j=PAIR), in_=z_rows[:])
+            return a5_acc
 
-        all_halves = range(HALVES)
         all_passes = range(NODE_PASSES)
+        both = list(range(PAIR))
+        V, S = "vector", "scalar"
 
-        def tile_by_tile(pairs):
-            return [(i, half, g) for i in tiles_of(pairs) for half in all_halves for g in all_passes]
+        def store(i, halves=(0, HALVES)):
+            cols = slice(halves[0] * BANK, halves[1] * BANK)
+            nc.sync.dma_start(
+                out=rows_of(out_0, i)[:, cols], in_=t5_rows_of[i // PAIR][:, i % PAIR, cols]
+            )
 
-        prepare_a(tiles_of(groups[0]))
-        for g in all_passes:
-            quantise_h(g)
-        first_matmul(
-            [(i, half, g) for g in all_passes for half in all_halves for i in tiles_of(groups[0])]
+        def multiply(tiles, engines):
+            for i in tiles:
+                for half in range(HALVES):
+                    first_matmul([(i, half, g) for g in all_passes], lambda i: engines[half])
+                store(i)
+
+        def flip_and_quantise(tiles, engines):
+            waiting = None
+            for i in tiles:
+                flip_a(i, engines if i % 2 else [S, S])
+                if waiting is not None:
+                    quantise_a(waiting)
+                waiting = i
+            quantise_a(waiting)
+
+        def flip_pair(p, engines):
+            for j in both:
+                flip_t(p, [(j, 0), (j, 1)], engines[j])
+
+        def round_pair(p):
+            t_rows = four.tile([P, PAIR, FEATS], BF16, tag="t_rows")
+            t_rows_of[p] = t_rows
+            nc.vector.tensor_copy(out=t_rows[:], in_=t5_rows_of[p][:])
+
+        results_of = {}
+
+        def put(p, tiles_in_pair, acc, is_z, engine):
+            count = len(tiles_in_pair)
+            key = (p, tiles_in_pair[0])
+            if key not in results_of:
+                results = five.tile([P, 2, PAIR, OUTS], F32, align_bytes=64, tag="row_tile")
+                results_of[key] = results
+            result = results_of[key][:, int(is_z), 0:count, :]
+            if is_z:
+                nc.scalar.activation(out=result, in_=acc[:], func=mybir.ActivationFunctionType.Sigmoid)
+            else:
+                copy_on(engine, result, acc[:])
+            out = out_2 if is_z else out_1
+            rows = out[p * PAIR * P : (p + 1) * PAIR * P, :].rearrange("(m j) n -> m j n", j=PAIR)
+            nc.sync.dma_start(out=rows[:, tiles_in_pair[0] : tiles_in_pair[0] + count, :], in_=result)
+
+        def put_a5(p, tiles_in_pair, acc, engine):
+            put(p, tiles_in_pair, acc, False, engine)
+
+        def put_z(p, tiles_in_pair, acc):
+            put(p, tiles_in_pair, acc, True, S)
+
+        load_a(0)
+        load_h(0)
+        load_a(1)
+        load_h(1)
+        load_a(2)
+        load_a(3)
+        load_h(2)
+        load_h(3)
+        for i in range(4, 8):
+            load_a(i)
+        w_rows = keep.tile([P, FEAT_PASSES, PACK, OUTS], BF16)
+        nc.sync.dma_start(
+            out=w_rows[:].rearrange("q g (u e) n -> q (g u) e n", e=2),
+            in_=W4.rearrange("(gu q e) n -> q gu e n", q=P, e=2),
         )
 
-        for n in range(1, len(groups)):
-            prepare_a(tiles_of(groups[n]))
-            if n >= 2:
-                prepare_t(groups[n - 2])
-            for p in groups[n - 1]:
-                round_t(p)
-            if n == 1:
-                quantise_w()
-            first_matmul(tile_by_tile(groups[n][:1]))
-            if n >= 2:
-                for p in groups[n - 2]:
-                    second_matmul(p)
-            first_matmul(tile_by_tile(groups[n][1:]))
+        def head(g, tiles, halves=range(HALVES)):
+            for half in halves:
+                first_matmul([(i, half, g) for i in tiles], lambda i: [V, S][i % 2])
 
-        for p in groups[-1]:
-            round_t(p)
-        prepare_t(groups[-2] + groups[-1])
-        for p in groups[-2] + groups[-1]:
-            second_matmul(p)
+        flip_a(0, [V, S])
+        group_h(0, V, 0, H_SPLIT)
+        group_h(0, S, H_SPLIT, FEATS)
+        quantise_a(0)
+        quantise_h(0, 0, 512)
+        quantise_h(0, 512, 1024)
+        flip_a(1, [S, S])
+        group_h(1, V, 0, H_SPLIT)
+        quantise_a(1)
+        group_h(1, S, H_SPLIT, FEATS)
+        head(0, [0])
+        flip_a(2, [S, S])
+        head(0, [1])
+        quantise_h(1, 0, 512)
+        quantise_h(1, 512, 1024)
+        flip_a(3, [V, S])
+        head(1, [0, 1])
+        quantise_a(2)
+        quantise_a(3)
+        group_h(2, V, 0, H_SPLIT)
+        group_h(2, S, H_SPLIT, FEATS)
+        head(0, [2, 3])
+        head(1, [2, 3])
+        quantise_h(2, 0, 512)
+        quantise_h(2, 512, 1024)
+        group_h(3, V, 0, H_SPLIT)
+        group_h(3, S, H_SPLIT, FEATS)
+        head(2, [0, 1, 2, 3])
+        quantise_h(3, 0, 512)
+        quantise_h(3, 512, 1024)
+        head(3, [0, 1, 2, 3])
+        for i in range(4):
+            store(i)
+        for i in range(8, 12):
+            load_a(i)
+
+        flip_and_quantise([4, 5, 6, 7], [V, S])
+        quantise_w()
+        for i in range(12, 16):
+            load_a(i)
+        multiply([4, 5], [S, V])
+        round_pair(0)
+        round_pair(1)
+        multiply([6, 7], [S, V])
+        flip_and_quantise([8, 9, 10, 11], [V, S])
+        flip_pair(0, [S, V])
+        flip_pair(1, [S, V])
+        quantise_t(0, 0, 4)
+        quantise_t(1, 0, 4)
+        multiply([8, 9], [S, S])
+        round_pair(2)
+        round_pair(3)
+        for p in (0, 1):
+            acc = second_matmul(p, both)
+            put_a5(p, both, acc, V)
+            put_z(p, both, acc)
+        multiply([10, 11], [S, S])
+        flip_and_quantise([12, 13, 14, 15], [V, S])
+        flip_pair(2, [S, V])
+        flip_pair(3, [S, V])
+        quantise_t(2, 0, 4)
+        quantise_t(3, 0, 4)
+        round_pair(4)
+        round_pair(5)
+        multiply([12, 13], [S, S])
+        for p in (2, 3):
+            acc = second_matmul(p, both)
+            put_a5(p, both, acc, V)
+            put_z(p, both, acc)
+        flip_pair(4, [S, V])
+        flip_pair(5, [S, V])
+        round_pair(6)
+        quantise_t(4, 0, 4)
+        quantise_t(5, 0, 4)
+        multiply([14], [S, S])
+        first_matmul([(15, 0, g) for g in all_passes], lambda i: S)
+        store(15, (0, 1))
+        round_t(7, 0, slice(0, 1))
+        round_t(7, 1, slice(0, 1))
+        accs = [second_matmul(p, both) for p in (4, 5)]
+        round_t(7, 0, slice(1, 2))
+        put_a5(4, both, accs[0], V)
+        flip_pair(6, [S, V])
+        put_z(4, both, accs[0])
+        flip_t(7, [(0, 0), (0, 1)], S)
+        flip_t(7, [(1, 0)], V)
+        put_z(5, both, accs[1])
+        put_a5(5, both, accs[1], S)
+        quantise_t(6, 0, 4)
+        first_matmul([(15, 1, g) for g in all_passes], lambda i: S, [15])
+        store(15, (1, 2))
+        quantise_t(7, 0, 2)
+        quantise_t(7, 2, 3)
+        acc6 = second_matmul(6, both)
+        put_z(6, both, acc6)
+        flip_t(7, [(1, 1)], V)
+        first_acc = second_matmul(7, [0])
+        quantise_t(7, 3, 4)
+        put_z(7, [0], first_acc)
+        put_a5(6, both, acc6, V)
+        last_acc = second_matmul(7, [1])
+        put_z(7, [1], last_acc)
+        put_a5(7, [0], first_acc, V)
+        put_a5(7, [1], last_acc, V)

@@ -76,10 +76,10 @@ def tile_gcn_kron_pb_kernel(tc, h4, A, W4, out_0, out_1, out_2):
             )
             h_rows_of[g] = h_rows
 
-        h_codes = keep.tile([P, NODE_PASSES, FEATS], U32, align_bytes=64)
-        h_scales = keep.tile([P, NODE_PASSES, FEATS], U8, align_bytes=64)
-        w_codes = keep.tile([P, FEAT_PASSES, OUTS], U32, align_bytes=64)
-        w_scales = keep.tile([P, FEAT_PASSES, OUTS], U8, align_bytes=64)
+        h_codes = keep.tile([P, NODE_PASSES, FEATS], U32, align_bytes=256)
+        h_scales = keep.tile([P, NODE_PASSES, FEATS], U8, align_bytes=256)
+        w_codes = keep.tile([P, FEAT_PASSES, OUTS], U32, align_bytes=256)
+        w_scales = keep.tile([P, FEAT_PASSES, OUTS], U8, align_bytes=256)
 
         def copy_on(engine, out, in_):
             if engine == "vector":
@@ -147,8 +147,8 @@ def tile_gcn_kron_pb_kernel(tc, h4, A, W4, out_0, out_1, out_2):
             transpose_pairs(a_rows_of[i][:], a_grouped[:], NODE_PASSES, engines)
 
         def quantise_a(i):
-            a_codes = six.tile([P, NODE_PASSES, P], U32, align_bytes=64)
-            a_scales = six.tile([P, NODE_PASSES, P], U8, align_bytes=64)
+            a_codes = six.tile([P, NODE_PASSES, P], U32, align_bytes=256)
+            a_scales = six.tile([P, NODE_PASSES, P], U8, align_bytes=256)
             nc.vector.quantize_mx(
                 out=a_codes[:].rearrange("q g m -> q (g m)").bitcast(FP8X4),
                 scales=a_scales[:].rearrange("q g m -> q (g m)"),
@@ -227,8 +227,8 @@ def tile_gcn_kron_pb_kernel(tc, h4, A, W4, out_0, out_1, out_2):
 
         def quantise_t(p, first, last):
             if p not in t_quantised_of:
-                t_codes = three.tile([P, PAIR * FEAT_PASSES, P], U32, align_bytes=64)
-                t_scales = three.tile([P, PAIR * FEAT_PASSES, P], U8, align_bytes=64)
+                t_codes = three.tile([P, PAIR * FEAT_PASSES, P], U32, align_bytes=256)
+                t_scales = three.tile([P, PAIR * FEAT_PASSES, P], U8, align_bytes=256)
                 t_quantised_of[p] = (t_codes, t_scales)
             t_codes, t_scales = t_quantised_of[p]
             nc.vector.quantize_mx(

@@ -179,7 +179,7 @@ def tile_gcn_kron_pb_kernel(tc, h4, A, W4, out_0, out_1, out_2):
                 )
                 if g == NODE_PASSES - 1 and i in round_from_sums:
                     round_t(i // PAIR, half, slice(i % PAIR, i % PAIR + 1), t5_acc_of[(i, half)][:])
-                if g == NODE_PASSES - 1:
+                if g == NODE_PASSES - 1 and engine_of(i) is not None:
                     copy_on(engine_of(i), t5_rows_of[i // PAIR][:, i % PAIR, cols], t5_acc_of[(i, half)][:])
 
         def store_t5(tiles, half):
@@ -284,7 +284,7 @@ def tile_gcn_kron_pb_kernel(tc, h4, A, W4, out_0, out_1, out_2):
         def flip_and_quantise(tiles, engines):
             waiting = None
             for i in tiles:
-                flip_a(i, engines if i % 2 else [S, S])
+                flip_a(i, [S, S] if i % 2 else engines)
                 if waiting is not None:
                     quantise_a(waiting)
                 waiting = i
@@ -322,6 +322,36 @@ def tile_gcn_kron_pb_kernel(tc, h4, A, W4, out_0, out_1, out_2):
         def put_z(p, tiles_in_pair, acc):
             put(p, tiles_in_pair, acc, True, S)
 
+        def last_tile():
+            t_codes, t_scales = t_quantised_of[ROW_TILES // PAIR - 1]
+            results = five.tile([P, 2, OUTS], F32, align_bytes=64, tag="row_tile")
+            halves = []
+            for first in (0, P):
+                acc = psum.tile([P, P], F32, tag="bank")
+                for g in range(FEAT_PASSES):
+                    slot = (PAIR - 1) * FEAT_PASSES + g
+                    nc.tensor.matmul_mx(
+                        out=acc[:],
+                        lhsT=t_codes[:, slot, :].bitcast(FP8X4),
+                        lhsT_scale=t_scales[:, slot, :],
+                        rhs=w_codes[:, g, first : first + P].bitcast(FP8X4),
+                        rhs_scale=w_scales[:, g, first : first + P],
+                        start=(g == 0),
+                        stop=(g == FEAT_PASSES - 1),
+                    )
+                halves.append((first, acc))
+            for vector_half, scalar_half in ((0, 1), (1, 0)):
+                first, acc = halves[vector_half]
+                nc.vector.tensor_copy(out=results[:, 0, first : first + P], in_=acc[:])
+                first, acc = halves[scalar_half]
+                nc.scalar.activation(
+                    out=results[:, 1, first : first + P],
+                    in_=acc[:],
+                    func=mybir.ActivationFunctionType.Sigmoid,
+                )
+            for out, k in ((out_1, 0), (out_2, 1)):
+                nc.sync.dma_start(out=rows_of(out, ROW_TILES - 1), in_=results[:, k, :])
+
         load_a(0)
         load_h(0)
         load_a(1)
@@ -353,11 +383,11 @@ def tile_gcn_kron_pb_kernel(tc, h4, A, W4, out_0, out_1, out_2):
         quantise_a(1)
         group_h(1, S, H_SPLIT, FEATS)
         head(0, [0])
-        flip_a(2, [S, S])
-        head(0, [1])
         quantise_h(1, 0, 512)
+        flip_a(2, [V, S])
+        flip_a(3, [S, S])
+        head(0, [1])
         quantise_h(1, 512, 1024)
-        flip_a(3, [V, S])
         head(1, [0, 1])
         quantise_a(2)
         quantise_a(3)
@@ -413,36 +443,33 @@ def tile_gcn_kron_pb_kernel(tc, h4, A, W4, out_0, out_1, out_2):
             put_z(p, both, acc)
         flip_pair(4, [S, V])
         flip_pair(5, [S, V])
-        round_pair(6)
         quantise_t(4, 0, 4)
         quantise_t(5, 0, 4)
+        round_pair(6)
         multiply([14], [S, S])
-        first_matmul([(15, 0, g) for g in all_passes], lambda i: S)
-        store(15, (0, 1))
+        accs = [second_matmul(p, both) for p in (4, 5)]
+        put_a5(4, both, accs[0], V)
+        put_z(5, both, accs[1])
         round_t(7, 0, slice(0, 1))
         round_t(7, 1, slice(0, 1))
-        accs = [second_matmul(p, both) for p in (4, 5)]
-        round_t(7, 0, slice(1, 2))
-        put_a5(4, both, accs[0], V)
-        flip_pair(6, [S, V])
         put_z(4, both, accs[0])
+        put_a5(5, both, accs[1], V)
+        first_matmul([(15, 0, g) for g in all_passes], lambda i: S)
+        store(15, (0, 1))
+        flip_pair(6, [S, V])
         flip_t(7, [(0, 0), (0, 1)], S)
-        flip_t(7, [(1, 0)], V)
-        put_z(5, both, accs[1])
-        put_a5(5, both, accs[1], S)
         quantise_t(6, 0, 4)
+        round_t(7, 0, slice(1, 2))
         first_matmul([(15, 1, g) for g in all_passes], lambda i: S, [15])
         store(15, (1, 2))
         quantise_t(7, 0, 2)
-        quantise_t(7, 2, 3)
         acc6 = second_matmul(6, both)
         put_z(6, both, acc6)
+        flip_t(7, [(1, 0)], V)
         flip_t(7, [(1, 1)], V)
         first_acc = second_matmul(7, [0])
-        quantise_t(7, 3, 4)
+        quantise_t(7, 2, 4)
         put_z(7, [0], first_acc)
         put_a5(6, both, acc6, V)
-        last_acc = second_matmul(7, [1])
-        put_z(7, [1], last_acc)
         put_a5(7, [0], first_acc, V)
-        put_a5(7, [1], last_acc, V)
+        last_tile()

@@ -27,7 +27,7 @@ HALVES = FEATS // BANK
 PAIR = 2
 GROUP_PAIRS = 2
 assert PAIR * OUTS == BANK
-H_SPLIT = 512
+H_PIECE = BANK // 2
 A_BUFFERS = 8
 
 FLOPS = 2 * NODES * NODES * FEATS + 2 * NODES * FEATS * OUTS
@@ -49,7 +49,7 @@ def tile_gcn_kron_pb_kernel(tc, h4, A, W4, out_0, out_1, out_2):
         three = ctx.enter_context(tc.tile_pool(name="three", bufs=3))
         four = ctx.enter_context(tc.tile_pool(name="four", bufs=4))
         five = ctx.enter_context(tc.tile_pool(name="five", bufs=5))
-        six = ctx.enter_context(tc.tile_pool(name="six", bufs=6))
+        nine = ctx.enter_context(tc.tile_pool(name="nine", bufs=9))
         psum = ctx.enter_context(tc.psum_pool(name="psum", bufs=8))
         ctx.enter_context(tc.manual_schedule())
 
@@ -68,13 +68,17 @@ def tile_gcn_kron_pb_kernel(tc, h4, A, W4, out_0, out_1, out_2):
             nc.sync.dma_start(out=a_rows[:], in_=rows_of(A, i))
             a_rows_of[i] = a_rows
 
-        def load_h(g):
-            h_rows = h_in.tile([P, PACK, FEATS], BF16)
-            nc.sync.dma_start(
-                out=h_rows[:].rearrange("q (u e) c -> q u e c", e=2),
-                in_=h4[g * K_PASS : (g + 1) * K_PASS, :].rearrange("(u q e) c -> q u e c", u=2, e=2),
-            )
-            h_rows_of[g] = h_rows
+        def load_h(g, half):
+            h_rows = h_in.tile([P, PACK, BANK], BF16, tag="h_rows")
+            for u in range(2):
+                first = g * K_PASS + u * 2 * P
+                nc.sync.dma_start(
+                    out=h_rows[:, 2 * u : 2 * u + 2, :],
+                    in_=h4[first : first + 2 * P, half * BANK : (half + 1) * BANK].rearrange(
+                        "(q e) c -> q e c", e=2
+                    ),
+                )
+            h_rows_of[(g, half)] = h_rows
 
         h_codes = keep.tile([P, NODE_PASSES, FEATS], U32, align_bytes=256)
         h_scales = keep.tile([P, NODE_PASSES, FEATS], U8, align_bytes=256)
@@ -89,21 +93,22 @@ def tile_gcn_kron_pb_kernel(tc, h4, A, W4, out_0, out_1, out_2):
 
         h_grouped_of = {}
 
-        def group_h(g, engine, first, last):
-            if g not in h_grouped_of:
-                h_grouped = two.tile([P, FEATS, PACK], BF16, align_bytes=64)
-                h_grouped_of[g] = h_grouped
+        def group_h(g, half, engine, first, last):
+            if (g, half) not in h_grouped_of:
+                h_grouped = two.tile([P, BANK, PACK], BF16, align_bytes=64)
+                h_grouped_of[(g, half)] = h_grouped
             copy_on(
                 engine,
-                h_grouped_of[g][:, first:last, :].rearrange("q (c i) t -> q c t i", i=4),
-                h_rows_of[g][:, :, first:last].rearrange("q t (c i) -> q c t i", i=4),
+                h_grouped_of[(g, half)][:, first:last, :].rearrange("q (c i) t -> q c t i", i=4),
+                h_rows_of[(g, half)][:, :, first:last].rearrange("q t (c i) -> q c t i", i=4),
             )
 
-        def quantise_h(g, first, last):
+        def quantise_h(g, half, first, last):
+            cols = slice(half * BANK + first, half * BANK + last)
             nc.vector.quantize_mx(
-                out=h_codes[:, g, first:last].bitcast(FP8X4),
-                scales=h_scales[:, g, first:last],
-                in_=h_grouped_of[g][:, first:last, :].rearrange("q c t -> q (c t)"),
+                out=h_codes[:, g, cols].bitcast(FP8X4),
+                scales=h_scales[:, g, cols],
+                in_=h_grouped_of[(g, half)][:, first:last, :].rearrange("q c t -> q (c t)"),
             )
 
         def quantise_w():
@@ -147,8 +152,8 @@ def tile_gcn_kron_pb_kernel(tc, h4, A, W4, out_0, out_1, out_2):
             transpose_pairs(a_rows_of[i][:], a_grouped[:], NODE_PASSES, engines)
 
         def quantise_a(i):
-            a_codes = six.tile([P, NODE_PASSES, P], U32, align_bytes=256)
-            a_scales = six.tile([P, NODE_PASSES, P], U8, align_bytes=256)
+            a_codes = nine.tile([P, NODE_PASSES, P], U32, align_bytes=256)
+            a_scales = nine.tile([P, NODE_PASSES, P], U8, align_bytes=256)
             nc.vector.quantize_mx(
                 out=a_codes[:].rearrange("q g m -> q (g m)").bitcast(FP8X4),
                 scales=a_scales[:].rearrange("q g m -> q (g m)"),
@@ -352,70 +357,90 @@ def tile_gcn_kron_pb_kernel(tc, h4, A, W4, out_0, out_1, out_2):
             for out, k in ((out_1, 0), (out_2, 1)):
                 nc.sync.dma_start(out=rows_of(out, ROW_TILES - 1), in_=results[:, k, :])
 
-        load_a(0)
-        load_h(0)
-        load_a(1)
-        load_h(1)
-        load_a(2)
-        load_a(3)
-        load_h(2)
-        load_h(3)
+        for i in range(4):
+            load_a(i)
+        for g in range(NODE_PASSES):
+            load_h(g, 0)
         for i in range(4, 8):
             load_a(i)
+
+        def head(g, half, tiles):
+            first_matmul([(i, half, g) for i in tiles], lambda i: [V, S][i % 2])
+
+        def lay_out_right(g):
+            group_h(g, 1, V, 0, 256)
+            group_h(g, 1, S, 256, BANK)
+
+        def quantise_piece(g, half, piece):
+            quantise_h(g, half, piece * H_PIECE, (piece + 1) * H_PIECE)
+
+        flip_a(0, [V, S])
+        flip_a(1, [S, S])
+        quantise_a(0)
+        flip_a(2, [V, S])
+        quantise_a(1)
+        flip_a(3, [S, S])
+        group_h(0, 0, V, 0, 384)
+        group_h(0, 0, S, 384, BANK)
+        quantise_a(2)
+        quantise_piece(0, 0, 0)
+        quantise_piece(0, 0, 1)
+        quantise_a(3)
+        head(0, 0, [0, 1, 2, 3])
+        group_h(1, 0, V, 0, 256)
+        group_h(1, 0, S, 256, BANK)
+        quantise_piece(1, 0, 1)
+        quantise_piece(1, 0, 0)
+        head(1, 0, [0, 1, 2, 3])
+        group_h(2, 0, V, 0, 256)
+        group_h(2, 0, S, 256, BANK)
+        quantise_piece(2, 0, 1)
+        quantise_piece(2, 0, 0)
+        head(2, 0, [0, 1, 2, 3])
+        group_h(3, 0, V, 0, 256)
+        group_h(3, 0, S, 256, BANK)
+        quantise_piece(3, 0, 1)
+        quantise_piece(3, 0, 0)
+        head(3, 0, [0, 1, 2, 3])
+        flip_a(4, [V, S])
+        for g in range(NODE_PASSES):
+            load_h(g, 1)
         w_rows = keep.tile([P, FEAT_PASSES, PACK, OUTS], BF16)
         nc.sync.dma_start(
             out=w_rows[:].rearrange("q g (u e) n -> q (g u) e n", e=2),
             in_=W4.rearrange("(gu q e) n -> q gu e n", q=P, e=2),
         )
-
-        def head(g, tiles, halves=range(HALVES)):
-            for half in halves:
-                first_matmul([(i, half, g) for i in tiles], lambda i: [V, S][i % 2])
-
-        flip_a(0, [V, S])
-        group_h(0, V, 0, H_SPLIT)
-        group_h(0, S, H_SPLIT, FEATS)
-        quantise_a(0)
-        quantise_h(0, 0, 512)
-        quantise_h(0, 512, 1024)
-        flip_a(1, [S, S])
-        group_h(1, V, 0, H_SPLIT)
-        quantise_a(1)
-        group_h(1, S, H_SPLIT, FEATS)
-        head(0, [0])
-        quantise_h(1, 0, 512)
-        flip_a(2, [V, S])
-        flip_a(3, [S, S])
-        head(0, [1])
-        quantise_h(1, 512, 1024)
-        head(1, [0, 1])
-        quantise_a(2)
-        quantise_a(3)
-        group_h(2, V, 0, H_SPLIT)
-        group_h(2, S, H_SPLIT, FEATS)
-        head(0, [2, 3])
-        head(1, [2, 3])
-        quantise_h(2, 0, 512)
-        quantise_h(2, 512, 1024)
-        group_h(3, V, 0, H_SPLIT)
-        group_h(3, S, H_SPLIT, FEATS)
-        head(2, [0, 1, 2, 3])
-        quantise_h(3, 0, 512)
-        quantise_h(3, 512, 1024)
-        head(3, [0, 1, 2, 3])
-        for i in range(4):
-            store(i)
         for i in range(8, 12):
             load_a(i)
 
-        flip_and_quantise([4, 5, 6, 7], [V, S])
-        quantise_w()
+        flip_a(5, [S, S])
+        quantise_a(4)
+        flip_a(6, [V, S])
+        quantise_a(5)
+        flip_a(7, [S, S])
+        quantise_a(6)
+        lay_out_right(0)
+        quantise_a(7)
         for i in range(12, 16):
             load_a(i)
-        multiply([4, 5], [S, V])
+        for i in range(4, 8):
+            first_matmul([(i, 0, g) for g in all_passes], lambda i: None)
+        for g in range(1, NODE_PASSES):
+            lay_out_right(g)
+            quantise_h(g - 1, 1, 0, BANK)
+        quantise_h(NODE_PASSES - 1, 1, 0, BANK)
+        for i in range(4, 8):
+            copy_on(S, t5_rows_of[i // PAIR][:, i % PAIR, 0:BANK], t5_acc_of[(i, 0)][:])
+        for g in all_passes:
+            head(g, 1, [0, 1, 2, 3])
+        for i in range(4):
+            store(i)
         round_pair(0)
         round_pair(1)
-        multiply([6, 7], [S, V])
+        quantise_w()
+        for i in range(4, 8):
+            first_matmul([(i, 1, g) for g in all_passes], lambda i: S)
+            store(i)
         flip_and_quantise([8, 9, 10, 11], [V, S])
         flip_pair(0, [S, V])
         flip_pair(1, [S, V])

from contextlib import ExitStack

import concourse.mybir as mybir
from concourse.masks import make_identity

F32 = mybir.dt.float32
BF16 = mybir.dt.bfloat16
U32 = mybir.dt.uint32
U8 = mybir.dt.uint8
FP8X4 = mybir.dt.float8_e4m3fn_x4

P = 128
PACK = 4
K_PASS = P * PACK
BANK = 512
PSUM_BANKS = 8
PASSES_PER_BANK = 2

NODES = 2048
FEATS = 1024
OUTS = 256

ROW_TILES = NODES // P
NODE_PASSES = NODES // K_PASS
FEAT_PASSES = FEATS // K_PASS
HALVES = FEATS // BANK
PAIR = 2
GROUP_PAIRS = 2
assert PAIR * OUTS == BANK
H_PIECE = BANK // 2
A_BUFFERS = 8

FLOPS = 2 * NODES * NODES * FEATS + 2 * NODES * FEATS * OUTS


def tiles_of(pairs):
    return [PAIR * p + j for p in pairs for j in range(PAIR)]


def tile_gcn_kron_pb_kernel(tc, h4, A, W4, out_0, out_1, out_2):
    nc = tc.nc
    all_pairs = list(range(ROW_TILES // PAIR))
    groups = [all_pairs[first : first + GROUP_PAIRS] for first in range(0, len(all_pairs), GROUP_PAIRS)]
    with ExitStack() as ctx:
        keep = ctx.enter_context(tc.tile_pool(name="keep", bufs=1))
        a_in = ctx.enter_context(tc.tile_pool(name="a_in", bufs=A_BUFFERS))
        h_in = ctx.enter_context(tc.tile_pool(name="h_in", bufs=NODE_PASSES))
        two = ctx.enter_context(tc.tile_pool(name="two", bufs=2))
        three = ctx.enter_context(tc.tile_pool(name="three", bufs=3))
        four = ctx.enter_context(tc.tile_pool(name="four", bufs=4))
        five = ctx.enter_context(tc.tile_pool(name="five", bufs=5))
        nine = ctx.enter_context(tc.tile_pool(name="nine", bufs=9))
        psum = ctx.enter_context(tc.psum_pool(name="psum", bufs=8))
        ctx.enter_context(tc.manual_schedule())

        identity = keep.tile([P, P], F32)
        make_identity(nc, identity[:])

        a_rows_of = {}
        h_rows_of = {}

        def rows_of(x, i):
            first = (i // PAIR) * PAIR * P
            return x[first : first + PAIR * P, :].rearrange("(m j) n -> m j n", j=PAIR)[:, i % PAIR, :]

        def load_a(i):
            a_rows = a_in.tile([P, NODES], BF16)
            nc.sync.dma_start(out=a_rows[:], in_=rows_of(A, i))
            a_rows_of[i] = a_rows

        def load_h(g, half):
            h_rows = h_in.tile([P, PACK, BANK], BF16, tag="h_rows")
            for u in range(2):
                first = g * K_PASS + u * 2 * P
                nc.sync.dma_start(
                    out=h_rows[:, 2 * u : 2 * u + 2, :],
                    in_=h4[first : first + 2 * P, half * BANK : (half + 1) * BANK].rearrange(
                        "(q e) c -> q e c", e=2
                    ),
                )
            h_rows_of[(g, half)] = h_rows

        h_codes = keep.tile([P, NODE_PASSES, FEATS], U32, align_bytes=256)
        h_scales = keep.tile([P, NODE_PASSES, FEATS], U8, align_bytes=256)
        w_codes = keep.tile([P, FEAT_PASSES, OUTS], U32, align_bytes=256)
        w_scales = keep.tile([P, FEAT_PASSES, OUTS], U8, align_bytes=256)

        def copy_on(engine, out, in_):
            if engine == "vector":
                nc.vector.tensor_copy(out=out, in_=in_)
            else:
                nc.scalar.copy(out=out, in_=in_)

        h_grouped_of = {}

        def group_h(g, half, engine, first, last):
            if (g, half) not in h_grouped_of:
                h_grouped = two.tile([P, BANK, PACK], BF16, align_bytes=64)
                h_grouped_of[(g, half)] = h_grouped
            copy_on(
                engine,
                h_grouped_of[(g, half)][:, first:last, :].rearrange("q (c i) t -> q c t i", i=4),
                h_rows_of[(g, half)][:, :, first:last].rearrange("q t (c i) -> q c t i", i=4),
            )

        def quantise_h(g, half, first, last):
            cols = slice(half * BANK + first, half * BANK + last)
            nc.vector.quantize_mx(
                out=h_codes[:, g, cols].bitcast(FP8X4),
                scales=h_scales[:, g, cols],
                in_=h_grouped_of[(g, half)][:, first:last, :].rearrange("q c t -> q (c t)"),
            )

        def quantise_w():
            w_grouped = five.tile([P, FEAT_PASSES, OUTS, PACK], BF16, align_bytes=64, tag="row_tile")
            for g in range(FEAT_PASSES):
                nc.vector.tensor_copy(
                    out=w_grouped[:, g, :, :], in_=w_rows[:, g, :, :].rearrange("q t n -> q n t")
                )
            nc.vector.quantize_mx(
                out=w_codes[:].rearrange("q g n -> q (g n)").bitcast(FP8X4),
                scales=w_scales[:].rearrange("q g n -> q (g n)"),
                in_=w_grouped[:].rearrange("q g n t -> q (g n t)"),
            )

        def transpose_pairs(rows, grouped, passes, engines):
            words = rows.bitcast(F32)
            grouped_words = grouped.bitcast(F32).rearrange("q (g m u) -> q g m u", g=passes, u=2)
            for bank in range(passes // PASSES_PER_BANK):
                flipped = psum.tile([P, 2 * PASSES_PER_BANK, P], F32, tag="bank")
                for j in range(2 * PASSES_PER_BANK):
                    block = bank * 2 * PASSES_PER_BANK + j
                    nc.tensor.transpose(
                        flipped[:, j, :], words[:, block * P : (block + 1) * P], identity[:]
                    )
                copy_on(
                    engines[bank],
                    grouped_words[:, bank * PASSES_PER_BANK : (bank + 1) * PASSES_PER_BANK, :, :],
                    flipped[:].rearrange("q (g u) m -> q g m u", u=2),
                )

        a_quantised_of = {}
        t5_rows_of = {}
        t_rows_of = {}
        t_quantised_of = {}

        a_grouped_of = {}

        def flip_a(i, engines):
            a_grouped = five.tile([P, NODES], BF16, align_bytes=64, tag="row_tile")
            a_grouped_of[i] = a_grouped
            transpose_pairs(a_rows_of[i][:], a_grouped[:], NODE_PASSES, engines)

        def quantise_a(i):
            a_codes = nine.tile([P, NODE_PASSES, P], U32, align_bytes=256)
            a_scales = nine.tile([P, NODE_PASSES, P], U8, align_bytes=256)
            nc.vector.quantize_mx(
                out=a_codes[:].rearrange("q g m -> q (g m)").bitcast(FP8X4),
                scales=a_scales[:].rearrange("q g m -> q (g m)"),
                in_=a_grouped_of[i][:],
            )
            a_quantised_of[i] = (a_codes, a_scales)

        t5_acc_of = {}

        def first_matmul(passes_in_order, engine_of, round_from_sums=()):
            for i, half, g in passes_in_order:
                cols = slice(half * BANK, (half + 1) * BANK)
                if g == 0:
                    t5_acc = psum.tile([P, BANK], F32, tag="bank")
                    t5_acc_of[(i, half)] = t5_acc
                if i // PAIR not in t5_rows_of:
                    t5_rows = four.tile([P, PAIR, FEATS], F32)
                    t5_rows_of[i // PAIR] = t5_rows
                a_codes, a_scales = a_quantised_of[i]
                nc.tensor.matmul_mx(
                    out=t5_acc_of[(i, half)][:],
                    lhsT=a_codes[:, g, :].bitcast(FP8X4),
                    lhsT_scale=a_scales[:, g, :],
                    rhs=h_codes[:, g, cols].bitcast(FP8X4),
                    rhs_scale=h_scales[:, g, cols],
                    start=(g == 0),
                    stop=(g == NODE_PASSES - 1),
                )
                if g == NODE_PASSES - 1 and i in round_from_sums:
                    round_t(i // PAIR, half, slice(i % PAIR, i % PAIR + 1), t5_acc_of[(i, half)][:])
                if g == NODE_PASSES - 1 and engine_of(i) is not None:
                    copy_on(engine_of(i), t5_rows_of[i // PAIR][:, i % PAIR, cols], t5_acc_of[(i, half)][:])

        def store_t5(tiles, half):
            cols = slice(half * BANK, (half + 1) * BANK)
            for i in tiles:
                nc.sync.dma_start(
                    out=rows_of(out_0, i)[:, cols], in_=t5_rows_of[i // PAIR][:, i % PAIR, cols]
                )

        def round_t(p, half, tiles_in_pair=slice(0, PAIR), t5=None):
            cols = slice(half * BANK, (half + 1) * BANK)
            if p not in t_rows_of:
                t_rows = four.tile([P, PAIR, FEATS], BF16)
                t_rows_of[p] = t_rows
            t_part = t_rows_of[p][:, tiles_in_pair, cols]
            if t5 is None:
                nc.vector.tensor_copy(out=t_part, in_=t5_rows_of[p][:, tiles_in_pair, cols])
            else:
                nc.vector.tensor_copy(out=t_part.rearrange("q j k -> q (j k)"), in_=t5)

        t_grouped_of = {}

        def flip_t(p, parts, engine):
            if p not in t_grouped_of:
                t_grouped = two.tile([P, PAIR, FEATS], BF16, align_bytes=64)
                t_grouped_of[p] = t_grouped
            words = t_rows_of[p][:].rearrange("q j k -> q (j k)").bitcast(F32)
            grouped_words = (
                t_grouped_of[p][:].rearrange("q j k -> q (j k)").bitcast(F32)
            ).rearrange("q (s m u) -> q s m u", s=PAIR * FEAT_PASSES, u=2)
            flipped = psum.tile([P, 2 * PASSES_PER_BANK, P], F32, tag="bank")
            slots = [j * FEAT_PASSES + half for j, half in parts]
            for k, slot in enumerate(slots):
                for u in range(2):
                    block = 2 * slot + u
                    nc.tensor.transpose(
                        flipped[:, 2 * k + u, :], words[:, block * P : (block + 1) * P], identity[:]
                    )
            step = slots[-1] - slots[0] if len(slots) > 1 else 1
            copy_on(
                engine,
                grouped_words[:, slots[0] : slots[-1] + 1 : step, :, :],
                flipped[:, 0 : 2 * len(slots), :].rearrange("q (s u) m -> q s m u", u=2),
            )

        def quantise_t(p, first, last):
            if p not in t_quantised_of:
                t_codes = three.tile([P, PAIR * FEAT_PASSES, P], U32, align_bytes=256)
                t_scales = three.tile([P, PAIR * FEAT_PASSES, P], U8, align_bytes=256)
                t_quantised_of[p] = (t_codes, t_scales)
            t_codes, t_scales = t_quantised_of[p]
            nc.vector.quantize_mx(
                out=t_codes[:, first:last, :].rearrange("q s m -> q (s m)").bitcast(FP8X4),
                scales=t_scales[:, first:last, :].rearrange("q s m -> q (s m)"),
                in_=t_grouped_of[p][:].rearrange("q j k -> q (j k)")[:, first * BANK : last * BANK],
            )

        def prepare_t(pairs, engines, quantise_last=True):
            waiting = None
            for p in pairs:
                for j in range(PAIR):
                    flip_t(p, [(j, 0), (j, 1)], engines[j])
                if waiting is not None:
                    quantise_t(waiting, 0, PAIR * FEAT_PASSES)
                waiting = p
            if quantise_last:
                quantise_t(waiting, 0, PAIR * FEAT_PASSES)

        def second_matmul(p, tiles_in_pair):
            t_codes, t_scales = t_quantised_of[p]
            a5_acc = psum.tile([P, len(tiles_in_pair), OUTS], F32, tag="bank")
            for k, j in enumerate(tiles_in_pair):
                for g in range(FEAT_PASSES):
                    slot = j * FEAT_PASSES + g
                    nc.tensor.matmul_mx(
                        out=a5_acc[:, k, :],
                        lhsT=t_codes[:, slot, :].bitcast(FP8X4),
                        lhsT_scale=t_scales[:, slot, :],
                        rhs=w_codes[:, g, :].bitcast(FP8X4),
                        rhs_scale=w_scales[:, g, :],
                        start=(g == 0),
                        stop=(g == FEAT_PASSES - 1),
                    )
            return a5_acc

        all_passes = range(NODE_PASSES)
        both = list(range(PAIR))
        V, S = "vector", "scalar"

        def store(i, halves=(0, HALVES)):
            cols = slice(halves[0] * BANK, halves[1] * BANK)
            nc.sync.dma_start(
                out=rows_of(out_0, i)[:, cols], in_=t5_rows_of[i // PAIR][:, i % PAIR, cols]
            )

        def multiply(tiles, engines):
            for i in tiles:
                for half in range(HALVES):
                    first_matmul([(i, half, g) for g in all_passes], lambda i: engines[half])
                store(i)

        def flip_and_quantise(tiles, engines):
            waiting = None
            for i in tiles:
                flip_a(i, [S, S] if i % 2 else engines)
                if waiting is not None:
                    quantise_a(waiting)
                waiting = i
            quantise_a(waiting)

        def flip_pair(p, engines):
            for j in both:
                flip_t(p, [(j, 0), (j, 1)], engines[j])

        def round_pair(p):
            t_rows = four.tile([P, PAIR, FEATS], BF16, tag="t_rows")
            t_rows_of[p] = t_rows
            nc.vector.tensor_copy(out=t_rows[:], in_=t5_rows_of[p][:])

        results_of = {}

        def put(p, tiles_in_pair, acc, is_z, engine):
            count = len(tiles_in_pair)
            key = (p, tiles_in_pair[0])
            if key not in results_of:
                results = five.tile([P, 2, PAIR, OUTS], F32, align_bytes=64, tag="row_tile")
                results_of[key] = results
            result = results_of[key][:, int(is_z), 0:count, :]
            if is_z:
                nc.scalar.activation(out=result, in_=acc[:], func=mybir.ActivationFunctionType.Sigmoid)
            else:
                copy_on(engine, result, acc[:])
            out = out_2 if is_z else out_1
            rows = out[p * PAIR * P : (p + 1) * PAIR * P, :].rearrange("(m j) n -> m j n", j=PAIR)
            nc.sync.dma_start(out=rows[:, tiles_in_pair[0] : tiles_in_pair[0] + count, :], in_=result)

        def put_a5(p, tiles_in_pair, acc, engine):
            put(p, tiles_in_pair, acc, False, engine)

        def put_z(p, tiles_in_pair, acc):
            put(p, tiles_in_pair, acc, True, S)

        def last_tile():
            t_codes, t_scales = t_quantised_of[ROW_TILES // PAIR - 1]
            results = five.tile([P, 2, OUTS], F32, align_bytes=64, tag="row_tile")
            halves = []
            for first in (0, P):
                acc = psum.tile([P, P], F32, tag="bank")
                for g in range(FEAT_PASSES):
                    slot = (PAIR - 1) * FEAT_PASSES + g
                    nc.tensor.matmul_mx(
                        out=acc[:],
                        lhsT=t_codes[:, slot, :].bitcast(FP8X4),
                        lhsT_scale=t_scales[:, slot, :],
                        rhs=w_codes[:, g, first : first + P].bitcast(FP8X4),
                        rhs_scale=w_scales[:, g, first : first + P],
                        start=(g == 0),
                        stop=(g == FEAT_PASSES - 1),
                    )
                halves.append((first, acc))
            for vector_half, scalar_half in ((0, 1), (1, 0)):
                first, acc = halves[vector_half]
                nc.vector.tensor_copy(out=results[:, 0, first : first + P], in_=acc[:])
                first, acc = halves[scalar_half]
                nc.scalar.activation(
                    out=results[:, 1, first : first + P],
                    in_=acc[:],
                    func=mybir.ActivationFunctionType.Sigmoid,
                )
            for out, k in ((out_1, 0), (out_2, 1)):
                nc.sync.dma_start(out=rows_of(out, ROW_TILES - 1), in_=results[:, k, :])

        for i in range(4):
            load_a(i)
        for g in range(NODE_PASSES):
            load_h(g, 0)
        for i in range(4, 8):
            load_a(i)

        def head(g, half, tiles):
            first_matmul([(i, half, g) for i in tiles], lambda i: [V, S][i % 2])

        def lay_out_right(g):
            group_h(g, 1, V, 0, 256)
            group_h(g, 1, S, 256, BANK)

        def quantise_piece(g, half, piece):
            quantise_h(g, half, piece * H_PIECE, (piece + 1) * H_PIECE)

        flip_a(0, [V, S])
        flip_a(1, [S, S])
        quantise_a(0)
        flip_a(2, [V, S])
        quantise_a(1)
        flip_a(3, [S, S])
        group_h(0, 0, V, 0, 384)
        group_h(0, 0, S, 384, BANK)
        quantise_a(2)
        quantise_piece(0, 0, 0)
        quantise_piece(0, 0, 1)
        quantise_a(3)
        head(0, 0, [0, 1, 2, 3])
        group_h(1, 0, V, 0, 256)
        group_h(1, 0, S, 256, BANK)
        quantise_piece(1, 0, 1)
        quantise_piece(1, 0, 0)
        head(1, 0, [0, 1, 2, 3])
        group_h(2, 0, V, 0, 256)
        group_h(2, 0, S, 256, BANK)
        quantise_piece(2, 0, 1)
        quantise_piece(2, 0, 0)
        head(2, 0, [0, 1, 2, 3])
        group_h(3, 0, V, 0, 256)
        group_h(3, 0, S, 256, BANK)
        quantise_piece(3, 0, 1)
        quantise_piece(3, 0, 0)
        head(3, 0, [0, 1, 2, 3])
        flip_a(4, [V, S])
        for g in range(NODE_PASSES):
            load_h(g, 1)
        w_rows = keep.tile([P, FEAT_PASSES, PACK, OUTS], BF16)
        nc.sync.dma_start(
            out=w_rows[:].rearrange("q g (u e) n -> q (g u) e n", e=2),
            in_=W4.rearrange("(gu q e) n -> q gu e n", q=P, e=2),
        )
        for i in range(8, 12):
            load_a(i)

        flip_a(5, [S, S])
        quantise_a(4)
        flip_a(6, [V, S])
        quantise_a(5)
        flip_a(7, [S, S])
        quantise_a(6)
        lay_out_right(0)
        quantise_a(7)
        for i in range(12, 16):
            load_a(i)
        for i in range(4, 8):
            first_matmul([(i, 0, g) for g in all_passes], lambda i: None)
        for g in range(1, NODE_PASSES):
            lay_out_right(g)
            quantise_h(g - 1, 1, 0, BANK)
        quantise_h(NODE_PASSES - 1, 1, 0, BANK)
        for i in range(4, 8):
            copy_on(S, t5_rows_of[i // PAIR][:, i % PAIR, 0:BANK], t5_acc_of[(i, 0)][:])
        for g in all_passes:
            head(g, 1, [0, 1, 2, 3])
        for i in range(4):
            store(i)
        round_pair(0)
        round_pair(1)
        quantise_w()
        for i in range(4, 8):
            first_matmul([(i, 1, g) for g in all_passes], lambda i: S)
            store(i)
        flip_and_quantise([8, 9, 10, 11], [V, S])
        flip_pair(0, [S, V])
        flip_pair(1, [S, V])
        quantise_t(0, 0, 4)
        quantise_t(1, 0, 4)
        multiply([8, 9], [S, S])
        round_pair(2)
        round_pair(3)
        for p in (0, 1):
            acc = second_matmul(p, both)
            put_a5(p, both, acc, V)
            put_z(p, both, acc)
        multiply([10, 11], [S, S])
        flip_and_quantise([12, 13, 14, 15], [V, S])
        flip_pair(2, [S, V])
        flip_pair(3, [S, V])
        quantise_t(2, 0, 4)
        quantise_t(3, 0, 4)
        round_pair(4)
        round_pair(5)
        multiply([12, 13], [S, S])
        for p in (2, 3):
            acc = second_matmul(p, both)
            put_a5(p, both, acc, V)
            put_z(p, both, acc)
        flip_pair(4, [S, V])
        flip_pair(5, [S, V])
        quantise_t(4, 0, 4)
        quantise_t(5, 0, 4)
        round_pair(6)
        multiply([14], [S, S])
        accs = [second_matmul(p, both) for p in (4, 5)]
        put_a5(4, both, accs[0], V)
        put_z(5, both, accs[1])
        round_t(7, 0, slice(0, 1))
        round_t(7, 1, slice(0, 1))
        put_z(4, both, accs[0])
        put_a5(5, both, accs[1], V)
        first_matmul([(15, 0, g) for g in all_passes], lambda i: S)
        store(15, (0, 1))
        flip_pair(6, [S, V])
        flip_t(7, [(0, 0), (0, 1)], S)
        quantise_t(6, 0, 4)
        round_t(7, 0, slice(1, 2))
        first_matmul([(15, 1, g) for g in all_passes], lambda i: S, [15])
        store(15, (1, 2))
        quantise_t(7, 0, 2)
        acc6 = second_matmul(6, both)
        put_z(6, both, acc6)
        flip_t(7, [(1, 0)], V)
        flip_t(7, [(1, 1)], V)
        first_acc = second_matmul(7, [0])
        quantise_t(7, 2, 4)
        put_z(7, [0], first_acc)
        put_a5(6, both, acc6, V)
        put_a5(7, [0], first_acc, V)
        last_tile()
